import numpy as np
import ml_dtypes


def mxq(x, axis, fmt="e4m3"):
    dtype, down = {"e4m3": (ml_dtypes.float8_e4m3fn, 7), "e5m2": (ml_dtypes.float8_e5m2, 14)}[fmt]
    v = np.moveaxis(np.asarray(x, np.float32).astype(ml_dtypes.bfloat16).astype(np.float64), axis, -1)
    blocks = v.reshape(v.shape[:-1] + (-1, 32))
    amax = np.abs(blocks).max(-1, keepdims=True)
    byte = np.maximum(np.where(amax > 0, np.frexp(amax)[1] - 1 + 127, 0) - down, 1)
    scale = np.exp2(byte - 127.0)
    codes = (blocks / scale).astype(np.float32).astype(dtype).astype(np.float64)
    return np.moveaxis((codes * scale).reshape(v.shape), -1, axis)


WIDE = False


def mx_kscale(k):
    if not WIDE:
        return np.ones(k)
    levels = np.array([10, -10, 5, -5, 0])
    a = np.random.permutation(np.resize(levels, k // 512 * 4)).reshape(k // 512, 4)
    idx = np.arange(k)
    return np.exp2(a[idx // 512, idx % 128 // 32])


BF16 = ml_dtypes.bfloat16


def bf(x):
    return np.asarray(x, np.float32).astype(BF16)


def f64(x):
    return np.asarray(x).astype(np.float64)


B, COND, D, H, K = 4096, 512, 2, 512, 256
KD = K * D


def setup_inputs():
    s = mx_kscale(COND)
    return {
        "x": bf(np.random.standard_normal((B, COND)) * s),
        "W1": bf(np.random.standard_normal((COND, H)) * 0.8 / np.sqrt(COND) / s[:, None]),
        "b1": bf(np.random.standard_normal(H) * 0.3),
        "Wpi": bf(np.random.standard_normal((H, K)) * 3.5 / np.sqrt(H)),
        "bpi": bf(np.random.standard_normal(K) * 0.5),
        "Wsig": bf(np.random.standard_normal((H, KD)) * 1.0 / np.sqrt(H)),
        "bsig": bf(np.random.standard_normal(KD) * 0.3),
        "Wmu": bf(np.random.standard_normal((H, KD)) * 1.5 / np.sqrt(H)),
        "bmu": bf(np.random.standard_normal(KD) * 0.3),
    }


def reference(x, W1, b1, Wpi, bpi, Wsig, bsig, Wmu, bmu):
    z_h = np.tanh((mxq(f64(x), 1, "e4m3") @ mxq(f64(W1), 0, "e4m3")) + f64(b1))
    zq = mxq(z_h, 1, "e4m3")
    logits = (zq @ mxq(f64(Wpi), 0, "e4m3")) + f64(bpi)
    e = np.exp(logits - logits.max(-1, keepdims=True))
    pi = e / e.sum(-1, keepdims=True)
    sigma_diag = np.exp((zq @ mxq(f64(Wsig), 0, "e4m3")) + f64(bsig)).reshape(x.shape[0], K, D)
    sigma = sigma_diag[..., :, None] * np.eye(D)
    mu = ((zq @ mxq(f64(Wmu), 0, "e4m3")) + f64(bmu)).reshape(x.shape[0], K, D)
    return pi, sigma, mu

@@ -1,0 +1,312 @@
+from contextlib import ExitStack
+
+import concourse.mybir as mybir
+from concourse.masks import make_identity
+
+F32 = mybir.dt.float32
+BF16 = mybir.dt.bfloat16
+U32 = mybir.dt.uint32
+U8 = mybir.dt.uint8
+FP8X4 = mybir.dt.float8_e4m3fn_x4
+ACT = mybir.ActivationFunctionType
+ALU = mybir.AluOpType
+AXIS = mybir.AxisListType
+
+P = 128
+PACK = 4
+BATCH = 4096
+COND = 512
+HID = 512
+COMP = 256
+KD = 512
+DIAG = 4 * COMP
+
+TILES = BATCH // P
+GROUP = 4
+GROUPS = TILES // GROUP
+COLS = GROUP * P
+VECTOR_EVERY = 3
+
+FLOPS = 2 * BATCH * (COND * HID + HID * (COMP + 2 * KD))
+
+
+def tile_mdn_pa_t_kernel(tc, x, W1, b1, Wpi, bpi, Wsig, bsig, Wmu, bmu, out_0, out_1, out_2):
+    nc = tc.nc
+    x_view = x.rearrange("(p t) k -> p t k", t=TILES)
+    pi_view = out_0.rearrange("(p t) k -> p t k", t=TILES)
+    sigma_view = out_1.rearrange("(p t) k i j -> p t (k i j)", t=TILES)
+    mu_view = out_2.rearrange("(p t) k d -> p t (k d)", t=TILES)
+
+    with ExitStack() as ctx:
+        const = ctx.enter_context(tc.tile_pool(name="const", bufs=1))
+        wstage = ctx.enter_context(tc.tile_pool(name="wstage", bufs=2))
+        xpool = ctx.enter_context(tc.tile_pool(name="xpool", bufs=GROUPS))
+        xq = ctx.enter_context(tc.tile_pool(name="xq", bufs=2))
+        zq = ctx.enter_context(tc.tile_pool(name="zq", bufs=2))
+        small = ctx.enter_context(tc.tile_pool(name="small", bufs=3))
+        outs = ctx.enter_context(tc.tile_pool(name="outs", bufs=3))
+        sig_pool = ctx.enter_context(tc.tile_pool(name="sig", bufs=4))
+        psum = ctx.enter_context(tc.psum_pool(name="psum", bufs=8))
+
+        w1_raw = const.tile([P, PACK, HID], BF16)
+        nc.sync.dma_start(
+            out=w1_raw[:].rearrange("q (u e) n -> q u e n", u=2),
+            in_=W1.rearrange("(u q e) n -> q u e n", u=2, e=2),
+        )
+        x_sb = {}
+
+        def load_x(g):
+            x_g = xpool.tile([P, GROUP, COND], BF16)
+            nc.sync.dma_start(out=x_g[:], in_=x_view[:, g * GROUP : (g + 1) * GROUP, :])
+            x_sb[g] = x_g
+
+        load_x(0)
+        b1_col = const.tile([P, PACK], BF16)
+        nc.sync.dma_start(out=b1_col[:], in_=b1.rearrange("(m t) -> m t", t=PACK))
+        load_x(1)
+        wpi_raw = const.tile([P, PACK, COMP], BF16)
+        nc.sync.dma_start(out=wpi_raw[:], in_=Wpi.rearrange("(p j) n -> p j n", j=PACK))
+        wmu_raw = const.tile([P, PACK, KD], BF16)
+        nc.sync.dma_start(out=wmu_raw[:], in_=Wmu.rearrange("(p j) n -> p j n", j=PACK))
+        wsig_raw = const.tile([P, PACK, KD], BF16)
+        nc.sync.dma_start(out=wsig_raw[:], in_=Wsig.rearrange("(p j) n -> p j n", j=PACK))
+        bsig_col = const.tile([P, KD // P], BF16)
+        with nc.allow_non_contiguous_dma(reason="512 bias values, one to a partition"):
+            nc.sync.dma_start(out=bsig_col[:], in_=bsig.rearrange("(j c) -> c j", c=P))
+        bpi_row = const.tile([P, COMP], BF16)
+        nc.sync.dma_start(out=bpi_row[:], in_=bpi.partition_broadcast(P))
+        bmu_row = const.tile([P, KD], BF16)
+        nc.sync.dma_start(out=bmu_row[:], in_=bmu.partition_broadcast(P))
+        for g in range(2, GROUPS):
+            load_x(g)
+
+        ident = const.tile([P, P], F32)
+        make_identity(nc, ident[:])
+        spread = const.tile([P, 2 * P], F32)
+        nc.vector.memset(spread[:], 0.0)
+        for i in range(2):
+            nc.vector.tensor_copy(
+                out=spread[:].rearrange("c (k q) -> c k q", q=4)[:, :, 3 * i],
+                in_=ident[:].rearrange("c (k i) -> c k i", i=2)[:, :, i],
+            )
+
+        w1_codes = const.tile([P, HID], U32, align_bytes=64)
+        w1_scales = const.tile([P, HID], U8, align_bytes=64)
+        w1_grouped = wstage.tile([P, PACK, P, PACK], BF16, align_bytes=64, tag="w_grouped")
+        nc.vector.tensor_copy(out=w1_grouped[:], in_=w1_raw[:].rearrange("q j (m t) -> q t m j", t=PACK))
+        nc.vector.quantize_mx(
+            out=w1_codes[:].bitcast(FP8X4),
+            scales=w1_scales[:],
+            in_=w1_grouped[:].rearrange("q t m j -> q (t m j)"),
+        )
+
+        def quantise_head_weight(raw, width, codes, scales):
+            w_grouped = wstage.tile([P, width, PACK], BF16, align_bytes=64, tag="w_grouped")
+            nc.vector.tensor_copy(out=w_grouped[:], in_=raw[:].rearrange("p j n -> p n j"))
+            nc.vector.quantize_mx(
+                out=codes[:].bitcast(FP8X4),
+                scales=scales[:],
+                in_=w_grouped[:].rearrange("p n j -> p (n j)"),
+            )
+
+        wpi_codes = const.tile([P, COMP], U32, align_bytes=64)
+        wpi_scales = const.tile([P, COMP], U8, align_bytes=64)
+        wmu_codes = const.tile([P, KD], U32, align_bytes=64)
+        wmu_scales = const.tile([P, KD], U8, align_bytes=64)
+        wsig_codes = const.tile([P, KD], U32, align_bytes=64)
+        wsig_scales = const.tile([P, KD], U8, align_bytes=64)
+
+        x_grouped = {}
+        x_mx = {}
+        z_planes = {}
+        z_grouped = {}
+        z_mx = {}
+        logits = {}
+        neg_max = {}
+        sums = {}
+        sd_t = {}
+
+        def transpose_x(g):
+            grouped = xq.tile([P, COLS, PACK], BF16, align_bytes=64)
+            words = grouped[:].rearrange("q c t -> q (c t)").bitcast(F32).rearrange("q (c u) -> q c u", u=2)
+            for pair in range(GROUP // 2):
+                bank = psum.tile([P, 2, 2, P], F32, tag="bank")
+                for u in range(2):
+                    for a in range(2):
+                        nc.tensor.transpose(
+                            out=bank[:, u, a, :],
+                            in_=x_sb[g][:, 2 * pair + a, :].bitcast(F32)[:, u * P : (u + 1) * P],
+                            identity=ident[:],
+                        )
+                nc.scalar.copy(
+                    out=words[:, pair * 2 * P : (pair + 1) * 2 * P, :],
+                    in_=bank[:].rearrange("q u a r -> q (a r) u"),
+                )
+            x_grouped[g] = grouped
+
+        def quantise_x(g):
+            codes = xq.tile([P, COLS], U32, align_bytes=64)
+            scales = xq.tile([P, COLS], U8, align_bytes=64)
+            nc.vector.quantize_mx(
+                out=codes[:].bitcast(FP8X4),
+                scales=scales[:],
+                in_=x_grouped[g][:].rearrange("q c t -> q (c t)"),
+            )
+            x_mx[g] = (codes, scales)
+
+        def hidden(g):
+            codes, scales = x_mx[g]
+            planes = zq.tile([P, PACK, COLS], BF16)
+            for t in range(PACK):
+                bank = psum.tile([P, COLS], F32, tag="bank")
+                nc.tensor.matmul_mx(
+                    out=bank[:],
+                    lhsT=w1_codes[:, t * P : (t + 1) * P].bitcast(FP8X4),
+                    lhsT_scale=w1_scales[:, t * P : (t + 1) * P],
+                    rhs=codes[:].bitcast(FP8X4),
+                    rhs_scale=scales[:],
+                    start=True,
+                    stop=True,
+                )
+                nc.scalar.activation(out=planes[:, t, :], in_=bank[:], func=ACT.Tanh, bias=b1_col[:, t : t + 1])
+            z_planes[g] = planes
+
+        def regroup_z(g):
+            grouped = zq.tile([P, COLS, PACK], BF16, align_bytes=64)
+            nc.vector.tensor_copy(out=grouped[:], in_=z_planes[g][:].rearrange("m t c -> m c t"))
+            z_grouped[g] = grouped
+
+        def quantise_z(g):
+            codes = zq.tile([P, COLS], U32, align_bytes=64)
+            scales = zq.tile([P, COLS], U8, align_bytes=64)
+            nc.vector.quantize_mx(
+                out=codes[:].bitcast(FP8X4),
+                scales=scales[:],
+                in_=z_grouped[g][:].rearrange("m c t -> m (c t)"),
+            )
+            z_mx[g] = (codes, scales)
+
+        def heads(g):
+            codes, scales = z_mx[g]
+            rows = slice(g * GROUP, (g + 1) * GROUP)
+            logit = outs.tile([P, GROUP, COMP], F32)
+            for pair in range(GROUP // 2):
+                bank = psum.tile([P, 2, COMP], F32, tag="bank")
+                for a in range(2):
+                    cols = slice((2 * pair + a) * P, (2 * pair + a + 1) * P)
+                    nc.tensor.matmul_mx(
+                        out=bank[:, a, :],
+                        lhsT=codes[:, cols].bitcast(FP8X4),
+                        lhsT_scale=scales[:, cols],
+                        rhs=wpi_codes[:].bitcast(FP8X4),
+                        rhs_scale=wpi_scales[:],
+                        start=True,
+                        stop=True,
+                    )
+                nc.vector.tensor_tensor(
+                    out=logit[:, 2 * pair : 2 * pair + 2, :],
+                    in0=bank[:],
+                    in1=bpi_row[:].unsqueeze(1).to_broadcast([P, 2, COMP]),
+                    op=ALU.add,
+                )
+            negated = small.tile([P, GROUP], F32)
+            nc.vector.tensor_reduce(out=negated[:], in_=logit[:], axis=AXIS.X, op=ALU.max, negate=True)
+            logits[g] = logit
+            neg_max[g] = negated
+            mu_sb = outs.tile([P, GROUP, KD], F32)
+            for a in range(GROUP):
+                cols = slice(a * P, (a + 1) * P)
+                bank = psum.tile([P, KD], F32, tag="bank")
+                nc.tensor.matmul_mx(
+                    out=bank[:],
+                    lhsT=codes[:, cols].bitcast(FP8X4),
+                    lhsT_scale=scales[:, cols],
+                    rhs=wmu_codes[:].bitcast(FP8X4),
+                    rhs_scale=wmu_scales[:],
+                    start=True,
+                    stop=True,
+                )
+                nc.vector.tensor_tensor(out=mu_sb[:, a, :], in0=bank[:], in1=bmu_row[:], op=ALU.add)
+            nc.sync.dma_start(out=mu_view[:, rows, :], in_=mu_sb[:])
+            sd = zq.tile([P, KD // P, COLS], F32)
+            for j in range(KD // P):
+                bank = psum.tile([P, COLS], F32, tag="bank")
+                nc.tensor.matmul_mx(
+                    out=bank[:],
+                    lhsT=wsig_codes[:, j * P : (j + 1) * P].bitcast(FP8X4),
+                    lhsT_scale=wsig_scales[:, j * P : (j + 1) * P],
+                    rhs=codes[:].bitcast(FP8X4),
+                    rhs_scale=scales[:],
+                    start=True,
+                    stop=True,
+                )
+                nc.scalar.activation(out=sd[:, j, :], in_=bank[:], func=ACT.Exp, bias=bsig_col[:, j : j + 1])
+            sd_t[g] = sd
+
+        def exp_pi(g):
+            total = small.tile([P, GROUP], F32)
+            for a in range(GROUP):
+                nc.scalar.activation(
+                    out=logits[g][:, a, :],
+                    in_=logits[g][:, a, :],
+                    func=ACT.Exp,
+                    bias=neg_max[g][:, a : a + 1],
+                    accum_out=total[:, a : a + 1],
+                )
+            sums[g] = total
+
+        def finish_pi(g):
+            inverse = small.tile([P, GROUP], F32)
+            nc.vector.reciprocal(out=inverse[:], in_=sums[g][:])
+            for a in range(GROUP):
+                nc.vector.tensor_scalar_mul(
+                    out=logits[g][:, a, :], in0=logits[g][:, a, :], scalar1=inverse[:, a : a + 1]
+                )
+            nc.sync.dma_start(out=pi_view[:, g * GROUP : (g + 1) * GROUP, :], in_=logits[g][:])
+
+        def spread_sigma(g):
+            for pair in range(GROUP // 2):
+                sigma_sb = sig_pool.tile([P, 2, DIAG], F32)
+                for a in range(2):
+                    cols = slice((2 * pair + a) * P, (2 * pair + a + 1) * P)
+                    for half in range(2):
+                        bank = psum.tile([P, 2, 2 * P], F32, tag="bank")
+                        for b in range(2):
+                            for side in range(2):
+                                nc.tensor.transpose(
+                                    out=bank[:, b, side * P : (side + 1) * P],
+                                    in_=sd_t[g][:, 2 * half + b, cols],
+                                    identity=spread[:, side * P : (side + 1) * P],
+                                )
+                        dest = sigma_sb[:, a, half * 4 * P : (half + 1) * 4 * P]
+                        number = 4 * pair + 2 * a + half
+                        if number % VECTOR_EVERY == 0:
+                            nc.vector.tensor_copy(out=dest, in_=bank[:].rearrange("r b n -> r (b n)"))
+                        else:
+                            nc.scalar.copy(out=dest, in_=bank[:].rearrange("r b n -> r (b n)"))
+                first = g * GROUP + 2 * pair
+                nc.sync.dma_start(out=sigma_view[:, first : first + 2, :], in_=sigma_sb[:])
+
+        for step in range(GROUPS + 3):
+            g_x, g_h, g_o, g_s = step, step - 1, step - 2, step - 3
+            if 0 <= g_o < GROUPS:
+                regroup_z(g_o)
+            if 0 <= g_h < GROUPS:
+                quantise_x(g_h)
+            if 0 <= g_o < GROUPS:
+                quantise_z(g_o)
+            if 0 <= g_s < GROUPS:
+                exp_pi(g_s)
+                spread_sigma(g_s)
+            if 0 <= g_x < GROUPS:
+                transpose_x(g_x)
+            if 0 <= g_s < GROUPS:
+                finish_pi(g_s)
+            if 0 <= g_h < GROUPS:
+                hidden(g_h)
+            if step == 1:
+                quantise_head_weight(wpi_raw, COMP, wpi_codes, wpi_scales)
+                quantise_head_weight(wmu_raw, KD, wmu_codes, wmu_scales)
+                quantise_head_weight(wsig_raw, KD, wsig_codes, wsig_scales)
+            if 0 <= g_o < GROUPS:
+                heads(g_o)

@@ -25,7 +25,7 @@ TILES = BATCH // P
 GROUP = 4
 GROUPS = TILES // GROUP
 COLS = GROUP * P
-VECTOR_EVERY = 3
+SCALAR_BANKS = 5
 
 FLOPS = 2 * BATCH * (COND * HID + HID * (COMP + 2 * KD))
 
@@ -48,11 +48,6 @@ def tile_mdn_pa_t_kernel(tc, x, W1, b1, Wpi, bpi, Wsig, bsig, Wmu, bmu, out_0, o
         sig_pool = ctx.enter_context(tc.tile_pool(name="sig", bufs=4))
         psum = ctx.enter_context(tc.psum_pool(name="psum", bufs=8))
 
-        w1_raw = const.tile([P, PACK, HID], BF16)
-        nc.sync.dma_start(
-            out=w1_raw[:].rearrange("q (u e) n -> q u e n", u=2),
-            in_=W1.rearrange("(u q e) n -> q u e n", u=2, e=2),
-        )
         x_sb = {}
 
         def load_x(g):
@@ -61,15 +56,20 @@ def tile_mdn_pa_t_kernel(tc, x, W1, b1, Wpi, bpi, Wsig, bsig, Wmu, bmu, out_0, o
             x_sb[g] = x_g
 
         load_x(0)
+        w1_raw = const.tile([P, PACK, HID], BF16)
+        nc.sync.dma_start(
+            out=w1_raw[:].rearrange("q (u e) n -> q u e n", u=2),
+            in_=W1.rearrange("(u q e) n -> q u e n", u=2, e=2),
+        )
         b1_col = const.tile([P, PACK], BF16)
         nc.sync.dma_start(out=b1_col[:], in_=b1.rearrange("(m t) -> m t", t=PACK))
         load_x(1)
         wpi_raw = const.tile([P, PACK, COMP], BF16)
         nc.sync.dma_start(out=wpi_raw[:], in_=Wpi.rearrange("(p j) n -> p j n", j=PACK))
-        wmu_raw = const.tile([P, PACK, KD], BF16)
-        nc.sync.dma_start(out=wmu_raw[:], in_=Wmu.rearrange("(p j) n -> p j n", j=PACK))
         wsig_raw = const.tile([P, PACK, KD], BF16)
         nc.sync.dma_start(out=wsig_raw[:], in_=Wsig.rearrange("(p j) n -> p j n", j=PACK))
+        wmu_raw = const.tile([P, PACK, KD], BF16)
+        nc.sync.dma_start(out=wmu_raw[:], in_=Wmu.rearrange("(p j) n -> p j n", j=PACK))
         bsig_col = const.tile([P, KD // P], BF16)
         with nc.allow_non_contiguous_dma(reason="512 bias values, one to a partition"):
             nc.sync.dma_start(out=bsig_col[:], in_=bsig.rearrange("(j c) -> c j", c=P))
@@ -92,13 +92,21 @@ def tile_mdn_pa_t_kernel(tc, x, W1, b1, Wpi, bpi, Wsig, bsig, Wmu, bmu, out_0, o
 
         w1_codes = const.tile([P, HID], U32, align_bytes=64)
         w1_scales = const.tile([P, HID], U8, align_bytes=64)
-        w1_grouped = wstage.tile([P, PACK, P, PACK], BF16, align_bytes=64, tag="w_grouped")
-        nc.vector.tensor_copy(out=w1_grouped[:], in_=w1_raw[:].rearrange("q j (m t) -> q t m j", t=PACK))
-        nc.vector.quantize_mx(
-            out=w1_codes[:].bitcast(FP8X4),
-            scales=w1_scales[:],
-            in_=w1_grouped[:].rearrange("q t m j -> q (t m j)"),
-        )
+        wpi_codes = const.tile([P, COMP], U32, align_bytes=64)
+        wpi_scales = const.tile([P, COMP], U8, align_bytes=64)
+        wmu_codes = const.tile([P, KD], U32, align_bytes=64)
+        wmu_scales = const.tile([P, KD], U8, align_bytes=64)
+        wsig_codes = const.tile([P, KD], U32, align_bytes=64)
+        wsig_scales = const.tile([P, KD], U8, align_bytes=64)
+
+        def quantise_w1():
+            w1_grouped = wstage.tile([P, PACK, P, PACK], BF16, align_bytes=64, tag="w_grouped")
+            nc.vector.tensor_copy(out=w1_grouped[:], in_=w1_raw[:].rearrange("q j (m t) -> q t m j", t=PACK))
+            nc.vector.quantize_mx(
+                out=w1_codes[:].bitcast(FP8X4),
+                scales=w1_scales[:],
+                in_=w1_grouped[:].rearrange("q t m j -> q (t m j)"),
+            )
 
         def quantise_head_weight(raw, width, codes, scales):
             w_grouped = wstage.tile([P, width, PACK], BF16, align_bytes=64, tag="w_grouped")
@@ -108,13 +116,6 @@ def tile_mdn_pa_t_kernel(tc, x, W1, b1, Wpi, bpi, Wsig, bsig, Wmu, bmu, out_0, o
                 scales=scales[:],
                 in_=w_grouped[:].rearrange("p n j -> p (n j)"),
             )
-
-        wpi_codes = const.tile([P, COMP], U32, align_bytes=64)
-        wpi_scales = const.tile([P, COMP], U8, align_bytes=64)
-        wmu_codes = const.tile([P, KD], U32, align_bytes=64)
-        wmu_scales = const.tile([P, KD], U8, align_bytes=64)
-        wsig_codes = const.tile([P, KD], U32, align_bytes=64)
-        wsig_scales = const.tile([P, KD], U8, align_bytes=64)
 
         x_grouped = {}
         x_mx = {}
@@ -154,22 +155,22 @@ def tile_mdn_pa_t_kernel(tc, x, W1, b1, Wpi, bpi, Wsig, bsig, Wmu, bmu, out_0, o
             )
             x_mx[g] = (codes, scales)
 
-        def hidden(g):
+        def hidden_bank(g, t):
             codes, scales = x_mx[g]
-            planes = zq.tile([P, PACK, COLS], BF16)
-            for t in range(PACK):
-                bank = psum.tile([P, COLS], F32, tag="bank")
-                nc.tensor.matmul_mx(
-                    out=bank[:],
-                    lhsT=w1_codes[:, t * P : (t + 1) * P].bitcast(FP8X4),
-                    lhsT_scale=w1_scales[:, t * P : (t + 1) * P],
-                    rhs=codes[:].bitcast(FP8X4),
-                    rhs_scale=scales[:],
-                    start=True,
-                    stop=True,
-                )
-                nc.scalar.activation(out=planes[:, t, :], in_=bank[:], func=ACT.Tanh, bias=b1_col[:, t : t + 1])
-            z_planes[g] = planes
+            if t == 0:
+                planes = zq.tile([P, PACK, COLS], BF16)
+                z_planes[g] = planes
+            bank = psum.tile([P, COLS], F32, tag="bank")
+            nc.tensor.matmul_mx(
+                out=bank[:],
+                lhsT=w1_codes[:, t * P : (t + 1) * P].bitcast(FP8X4),
+                lhsT_scale=w1_scales[:, t * P : (t + 1) * P],
+                rhs=codes[:].bitcast(FP8X4),
+                rhs_scale=scales[:],
+                start=True,
+                stop=True,
+            )
+            nc.scalar.activation(out=z_planes[g][:, t, :], in_=bank[:], func=ACT.Tanh, bias=b1_col[:, t : t + 1])
 
         def regroup_z(g):
             grouped = zq.tile([P, COLS, PACK], BF16, align_bytes=64)
@@ -186,36 +187,53 @@ def tile_mdn_pa_t_kernel(tc, x, W1, b1, Wpi, bpi, Wsig, bsig, Wmu, bmu, out_0, o
             )
             z_mx[g] = (codes, scales)
 
-        def heads(g):
+        def logit_bank(g, pair):
+            codes, scales = z_mx[g]
+            if pair == 0:
+                logit = outs.tile([P, GROUP, COMP], F32)
+                logits[g] = logit
+            bank = psum.tile([P, 2, COMP], F32, tag="bank")
+            for a in range(2):
+                cols = slice((2 * pair + a) * P, (2 * pair + a + 1) * P)
+                nc.tensor.matmul_mx(
+                    out=bank[:, a, :],
+                    lhsT=codes[:, cols].bitcast(FP8X4),
+                    lhsT_scale=scales[:, cols],
+                    rhs=wpi_codes[:].bitcast(FP8X4),
+                    rhs_scale=wpi_scales[:],
+                    start=True,
+                    stop=True,
+                )
+            nc.vector.tensor_tensor(
+                out=logits[g][:, 2 * pair : 2 * pair + 2, :],
+                in0=bank[:],
+                in1=bpi_row[:].unsqueeze(1).to_broadcast([P, 2, COMP]),
+                op=ALU.add,
+            )
+
+        def row_max(g):
+            negated = small.tile([P, GROUP], F32)
+            nc.vector.tensor_reduce(out=negated[:], in_=logits[g][:], axis=AXIS.X, op=ALU.max, negate=True)
+            neg_max[g] = negated
+
+        def sd_and_mu(g):
             codes, scales = z_mx[g]
             rows = slice(g * GROUP, (g + 1) * GROUP)
-            logit = outs.tile([P, GROUP, COMP], F32)
-            for pair in range(GROUP // 2):
-                bank = psum.tile([P, 2, COMP], F32, tag="bank")
-                for a in range(2):
-                    cols = slice((2 * pair + a) * P, (2 * pair + a + 1) * P)
-                    nc.tensor.matmul_mx(
-                        out=bank[:, a, :],
-                        lhsT=codes[:, cols].bitcast(FP8X4),
-                        lhsT_scale=scales[:, cols],
-                        rhs=wpi_codes[:].bitcast(FP8X4),
-                        rhs_scale=wpi_scales[:],
-                        start=True,
-                        stop=True,
-                    )
-                nc.vector.tensor_tensor(
-                    out=logit[:, 2 * pair : 2 * pair + 2, :],
-                    in0=bank[:],
-                    in1=bpi_row[:].unsqueeze(1).to_broadcast([P, 2, COMP]),
-                    op=ALU.add,
-                )
-            negated = small.tile([P, GROUP], F32)
-            nc.vector.tensor_reduce(out=negated[:], in_=logit[:], axis=AXIS.X, op=ALU.max, negate=True)
-            logits[g] = logit
-            neg_max[g] = negated
+            sd = zq.tile([P, KD // P, COLS], F32)
             mu_sb = outs.tile([P, GROUP, KD], F32)
             for a in range(GROUP):
                 cols = slice(a * P, (a + 1) * P)
+                bank = psum.tile([P, COLS], F32, tag="bank")
+                nc.tensor.matmul_mx(
+                    out=bank[:],
+                    lhsT=wsig_codes[:, cols].bitcast(FP8X4),
+                    lhsT_scale=wsig_scales[:, cols],
+                    rhs=codes[:].bitcast(FP8X4),
+                    rhs_scale=scales[:],
+                    start=True,
+                    stop=True,
+                )
+                nc.scalar.activation(out=sd[:, a, :], in_=bank[:], func=ACT.Exp, bias=bsig_col[:, a : a + 1])
                 bank = psum.tile([P, KD], F32, tag="bank")
                 nc.tensor.matmul_mx(
                     out=bank[:],
@@ -228,19 +246,6 @@ def tile_mdn_pa_t_kernel(tc, x, W1, b1, Wpi, bpi, Wsig, bsig, Wmu, bmu, out_0, o
                 )
                 nc.vector.tensor_tensor(out=mu_sb[:, a, :], in0=bank[:], in1=bmu_row[:], op=ALU.add)
             nc.sync.dma_start(out=mu_view[:, rows, :], in_=mu_sb[:])
-            sd = zq.tile([P, KD // P, COLS], F32)
-            for j in range(KD // P):
-                bank = psum.tile([P, COLS], F32, tag="bank")
-                nc.tensor.matmul_mx(
-                    out=bank[:],
-                    lhsT=wsig_codes[:, j * P : (j + 1) * P].bitcast(FP8X4),
-                    lhsT_scale=wsig_scales[:, j * P : (j + 1) * P],
-                    rhs=codes[:].bitcast(FP8X4),
-                    rhs_scale=scales[:],
-                    start=True,
-                    stop=True,
-                )
-                nc.scalar.activation(out=sd[:, j, :], in_=bank[:], func=ACT.Exp, bias=bsig_col[:, j : j + 1])
             sd_t[g] = sd
 
         def exp_pi(g):
@@ -280,33 +285,44 @@ def tile_mdn_pa_t_kernel(tc, x, W1, b1, Wpi, bpi, Wsig, bsig, Wmu, bmu, out_0, o
                                 )
                         dest = sigma_sb[:, a, half * 4 * P : (half + 1) * 4 * P]
                         number = 4 * pair + 2 * a + half
-                        if number % VECTOR_EVERY == 0:
+                        if number >= SCALAR_BANKS:
                             nc.vector.tensor_copy(out=dest, in_=bank[:].rearrange("r b n -> r (b n)"))
                         else:
                             nc.scalar.copy(out=dest, in_=bank[:].rearrange("r b n -> r (b n)"))
                 first = g * GROUP + 2 * pair
                 nc.sync.dma_start(out=sigma_view[:, first : first + 2, :], in_=sigma_sb[:])
 
-        for step in range(GROUPS + 3):
-            g_x, g_h, g_o, g_s = step, step - 1, step - 2, step - 3
-            if 0 <= g_o < GROUPS:
-                regroup_z(g_o)
-            if 0 <= g_h < GROUPS:
-                quantise_x(g_h)
-            if 0 <= g_o < GROUPS:
-                quantise_z(g_o)
-            if 0 <= g_s < GROUPS:
-                exp_pi(g_s)
-                spread_sigma(g_s)
-            if 0 <= g_x < GROUPS:
-                transpose_x(g_x)
-            if 0 <= g_s < GROUPS:
-                finish_pi(g_s)
-            if 0 <= g_h < GROUPS:
-                hidden(g_h)
-            if step == 1:
+        def live(g):
+            return 0 <= g < GROUPS
+
+        ctx.enter_context(tc.manual_schedule())
+        transpose_x(0)
+        quantise_w1()
+        quantise_x(0)
+        transpose_x(1)
+        for step in range(GROUPS + 1):
+            for t in range(PACK):
+                if live(step):
+                    hidden_bank(step, t)
+                if t < GROUP // 2 and live(step - 1):
+                    logit_bank(step - 1, t)
+            if step == 0:
                 quantise_head_weight(wpi_raw, COMP, wpi_codes, wpi_scales)
-                quantise_head_weight(wmu_raw, KD, wmu_codes, wmu_scales)
                 quantise_head_weight(wsig_raw, KD, wsig_codes, wsig_scales)
-            if 0 <= g_o < GROUPS:
-                heads(g_o)
+            if live(step - 1):
+                row_max(step - 1)
+                sd_and_mu(step - 1)
+                exp_pi(step - 1)
+            if live(step):
+                regroup_z(step)
+            if live(step + 1):
+                quantise_x(step + 1)
+            if live(step):
+                quantise_z(step)
+            if step == 0:
+                quantise_head_weight(wmu_raw, KD, wmu_codes, wmu_scales)
+            if live(step - 1):
+                finish_pi(step - 1)
+                spread_sigma(step - 1)
+            if live(step + 2):
+                transpose_x(step + 2)

@@ -25,7 +25,7 @@ TILES = BATCH // P
 GROUP = 4
 GROUPS = TILES // GROUP
 COLS = GROUP * P
-SCALAR_BANKS = 5
+SCALAR_BANKS = 4
 
 FLOPS = 2 * BATCH * (COND * HID + HID * (COMP + 2 * KD))
 

@@ -25,7 +25,7 @@ TILES = BATCH // P
 GROUP = 4
 GROUPS = TILES // GROUP
 COLS = GROUP * P
-SCALAR_BANKS = 4
+SCALAR_BANKS = 5
 
 FLOPS = 2 * BATCH * (COND * HID + HID * (COMP + 2 * KD))
 
@@ -174,7 +174,14 @@ def tile_mdn_pa_t_kernel(tc, x, W1, b1, Wpi, bpi, Wsig, bsig, Wmu, bmu, out_0, o
 
         def regroup_z(g):
             grouped = zq.tile([P, COLS, PACK], BF16, align_bytes=64)
-            nc.vector.tensor_copy(out=grouped[:], in_=z_planes[g][:].rearrange("m t c -> m c t"))
+            nc.gpsimd.tensor_scalar(
+                out=grouped[:],
+                in0=z_planes[g][:].rearrange("m t c -> m c t"),
+                scalar1=1.0,
+                scalar2=0.0,
+                op0=ALU.mult,
+                op1=ALU.add,
+            )
             z_grouped[g] = grouped
 
         def quantise_z(g):
@@ -264,8 +271,13 @@ def tile_mdn_pa_t_kernel(tc, x, W1, b1, Wpi, bpi, Wsig, bsig, Wmu, bmu, out_0, o
             inverse = small.tile([P, GROUP], F32)
             nc.vector.reciprocal(out=inverse[:], in_=sums[g][:])
             for a in range(GROUP):
-                nc.vector.tensor_scalar_mul(
-                    out=logits[g][:, a, :], in0=logits[g][:, a, :], scalar1=inverse[:, a : a + 1]
+                nc.gpsimd.tensor_scalar(
+                    out=logits[g][:, a, :],
+                    in0=logits[g][:, a, :],
+                    scalar1=inverse[:, a : a + 1],
+                    scalar2=0.0,
+                    op0=ALU.mult,
+                    op1=ALU.add,
                 )
             nc.sync.dma_start(out=pi_view[:, g * GROUP : (g + 1) * GROUP, :], in_=logits[g][:])
 

@@ -25,7 +25,7 @@ TILES = BATCH // P
 GROUP = 4
 GROUPS = TILES // GROUP
 COLS = GROUP * P
-SCALAR_BANKS = 5
+SCALAR_BANKS = (0, 2, 4, 6)
 
 FLOPS = 2 * BATCH * (COND * HID + HID * (COMP + 2 * KD))
 
@@ -297,7 +297,7 @@ def tile_mdn_pa_t_kernel(tc, x, W1, b1, Wpi, bpi, Wsig, bsig, Wmu, bmu, out_0, o
                                 )
                         dest = sigma_sb[:, a, half * 4 * P : (half + 1) * 4 * P]
                         number = 4 * pair + 2 * a + half
-                        if number >= SCALAR_BANKS:
+                        if number not in SCALAR_BANKS:
                             nc.vector.tensor_copy(out=dest, in_=bank[:].rearrange("r b n -> r (b n)"))
                         else:
                             nc.scalar.copy(out=dest, in_=bank[:].rearrange("r b n -> r (b n)"))

@@ -22,10 +22,9 @@ KD = 512
 DIAG = 4 * COMP
 
 TILES = BATCH // P
-GROUP = 4
-GROUPS = TILES // GROUP
-COLS = GROUP * P
-SCALAR_BANKS = (0, 2, 4, 6)
+SIZES = (2, 4, 4, 4, 4, 4, 4, 4, 2)
+FIRSTS = tuple(sum(SIZES[:g]) for g in range(len(SIZES)))
+GROUPS = len(SIZES)
 
 FLOPS = 2 * BATCH * (COND * HID + HID * (COMP + 2 * KD))
 
@@ -39,44 +38,43 @@ def tile_mdn_pa_t_kernel(tc, x, W1, b1, Wpi, bpi, Wsig, bsig, Wmu, bmu, out_0, o
 
     with ExitStack() as ctx:
         const = ctx.enter_context(tc.tile_pool(name="const", bufs=1))
-        wstage = ctx.enter_context(tc.tile_pool(name="wstage", bufs=2))
+        wstage = ctx.enter_context(tc.tile_pool(name="wstage", bufs=4))
         xpool = ctx.enter_context(tc.tile_pool(name="xpool", bufs=GROUPS))
-        xq = ctx.enter_context(tc.tile_pool(name="xq", bufs=2))
+        xq = ctx.enter_context(tc.tile_pool(name="xq", bufs=4))
         zq = ctx.enter_context(tc.tile_pool(name="zq", bufs=2))
         small = ctx.enter_context(tc.tile_pool(name="small", bufs=3))
         outs = ctx.enter_context(tc.tile_pool(name="outs", bufs=3))
-        sig_pool = ctx.enter_context(tc.tile_pool(name="sig", bufs=4))
+        sig_pool = ctx.enter_context(tc.tile_pool(name="sig", bufs=8))
+        rows_pool = ctx.enter_context(tc.tile_pool(name="rows", bufs=4))
         psum = ctx.enter_context(tc.psum_pool(name="psum", bufs=8))
 
         x_sb = {}
 
         def load_x(g):
-            x_g = xpool.tile([P, GROUP, COND], BF16)
-            nc.sync.dma_start(out=x_g[:], in_=x_view[:, g * GROUP : (g + 1) * GROUP, :])
+            x_g = xpool.tile([P, SIZES[g], COND], BF16)
+            nc.sync.dma_start(out=x_g[:], in_=x_view[:, FIRSTS[g] : FIRSTS[g] + SIZES[g], :])
             x_sb[g] = x_g
 
-        load_x(0)
         w1_raw = const.tile([P, PACK, HID], BF16)
         nc.sync.dma_start(
             out=w1_raw[:].rearrange("q (u e) n -> q u e n", u=2),
             in_=W1.rearrange("(u q e) n -> q u e n", u=2, e=2),
         )
+        load_x(0)
         b1_col = const.tile([P, PACK], BF16)
         nc.sync.dma_start(out=b1_col[:], in_=b1.rearrange("(m t) -> m t", t=PACK))
-        load_x(1)
-        wpi_raw = const.tile([P, PACK, COMP], BF16)
-        nc.sync.dma_start(out=wpi_raw[:], in_=Wpi.rearrange("(p j) n -> p j n", j=PACK))
-        wsig_raw = const.tile([P, PACK, KD], BF16)
-        nc.sync.dma_start(out=wsig_raw[:], in_=Wsig.rearrange("(p j) n -> p j n", j=PACK))
+        bias_rows = const.tile([P, 2 * KD + COMP], BF16)
+        nc.vector.memset(bias_rows[:], 0.0)
+        nc.sync.dma_start(out=bias_rows[0:1, 0:KD], in_=bsig.rearrange("(o n) -> o n", o=1))
+        nc.sync.dma_start(out=bias_rows[0:1, KD : 2 * KD], in_=bmu.rearrange("(o n) -> o n", o=1))
+        nc.sync.dma_start(out=bias_rows[0:1, 2 * KD :], in_=bpi.rearrange("(o n) -> o n", o=1))
         wmu_raw = const.tile([P, PACK, KD], BF16)
         nc.sync.dma_start(out=wmu_raw[:], in_=Wmu.rearrange("(p j) n -> p j n", j=PACK))
-        bsig_col = const.tile([P, KD // P], BF16)
-        with nc.allow_non_contiguous_dma(reason="512 bias values, one to a partition"):
-            nc.sync.dma_start(out=bsig_col[:], in_=bsig.rearrange("(j c) -> c j", c=P))
-        bpi_row = const.tile([P, COMP], BF16)
-        nc.sync.dma_start(out=bpi_row[:], in_=bpi.partition_broadcast(P))
-        bmu_row = const.tile([P, KD], BF16)
-        nc.sync.dma_start(out=bmu_row[:], in_=bmu.partition_broadcast(P))
+        load_x(1)
+        wsig_raw = const.tile([P, PACK, KD], BF16)
+        nc.sync.dma_start(out=wsig_raw[:], in_=Wsig.rearrange("(p j) n -> p j n", j=PACK))
+        wpi_raw = const.tile([P, PACK, COMP], BF16)
+        nc.sync.dma_start(out=wpi_raw[:], in_=Wpi.rearrange("(p j) n -> p j n", j=PACK))
         for g in range(2, GROUPS):
             load_x(g)
 
@@ -90,6 +88,36 @@ def tile_mdn_pa_t_kernel(tc, x, W1, b1, Wpi, bpi, Wsig, bsig, Wmu, bmu, out_0, o
                 in_=ident[:].rearrange("c (k i) -> c k i", i=2)[:, :, i],
             )
 
+        diagonals = []
+        for i in range(4):
+            diag = const.tile([P, DIAG], F32, name=f"diag{i}")
+            nc.gpsimd.memset(diag[:], 0.0)
+            diagonals.append(diag)
+
+        ones = const.tile([P, P], BF16)
+        nc.vector.memset(ones[:], 1.0)
+        bsig_row = const.tile([P, KD], BF16)
+        bmu_row = const.tile([P, KD], BF16)
+        bpi_row = const.tile([P, COMP], BF16)
+        bsig_col = const.tile([P, KD // P], F32)
+
+        def spread_bias(row, first, width):
+            bank = psum.tile([P, width], F32, tag="bank")
+            nc.tensor.matmul(out=bank[:], lhsT=ones[:], rhs=bias_rows[:, first : first + width], start=True, stop=True)
+            nc.scalar.copy(out=row[:], in_=bank[:])
+
+        def turn_bias():
+            bank = psum.tile([P, KD // P], F32, tag="bank")
+            for j in range(KD // P):
+                nc.tensor.matmul(
+                    out=bank[:, j : j + 1],
+                    lhsT=bias_rows[:, j * P : (j + 1) * P],
+                    rhs=ones[:, 0:1],
+                    start=True,
+                    stop=True,
+                )
+            nc.scalar.copy(out=bsig_col[:], in_=bank[:])
+
         w1_codes = const.tile([P, HID], U32, align_bytes=64)
         w1_scales = const.tile([P, HID], U8, align_bytes=64)
         wpi_codes = const.tile([P, COMP], U32, align_bytes=64)
@@ -98,6 +126,8 @@ def tile_mdn_pa_t_kernel(tc, x, W1, b1, Wpi, bpi, Wsig, bsig, Wmu, bmu, out_0, o
         wmu_scales = const.tile([P, KD], U8, align_bytes=64)
         wsig_codes = const.tile([P, KD], U32, align_bytes=64)
         wsig_scales = const.tile([P, KD], U8, align_bytes=64)
+
+        w_staged = {}
 
         def quantise_w1():
             w1_grouped = wstage.tile([P, PACK, P, PACK], BF16, align_bytes=64, tag="w_grouped")
@@ -108,9 +138,19 @@ def tile_mdn_pa_t_kernel(tc, x, W1, b1, Wpi, bpi, Wsig, bsig, Wmu, bmu, out_0, o
                 in_=w1_grouped[:].rearrange("q t m j -> q (t m j)"),
             )
 
-        def quantise_head_weight(raw, width, codes, scales):
+        def regroup_head_weight(name, raw, width, engine):
             w_grouped = wstage.tile([P, width, PACK], BF16, align_bytes=64, tag="w_grouped")
-            nc.vector.tensor_copy(out=w_grouped[:], in_=raw[:].rearrange("p j n -> p n j"))
+            view = raw[:].rearrange("p j n -> p n j")
+            if engine == "v":
+                nc.vector.tensor_copy(out=w_grouped[:], in_=view)
+            elif engine == "s":
+                nc.scalar.copy(out=w_grouped[:], in_=view)
+            else:
+                nc.gpsimd.tensor_scalar(out=w_grouped[:], in0=view, scalar1=1.0, scalar2=0.0, op0=ALU.mult, op1=ALU.add)
+            w_staged[name] = w_grouped
+
+        def quantise_head_weight(name, codes, scales):
+            w_grouped = w_staged[name]
             nc.vector.quantize_mx(
                 out=codes[:].bitcast(FP8X4),
                 scales=scales[:],
@@ -126,11 +166,13 @@ def tile_mdn_pa_t_kernel(tc, x, W1, b1, Wpi, bpi, Wsig, bsig, Wmu, bmu, out_0, o
         neg_max = {}
         sums = {}
         sd_t = {}
+        mu_out = {}
+        sd_row = {}
 
         def transpose_x(g):
-            grouped = xq.tile([P, COLS, PACK], BF16, align_bytes=64)
+            grouped = xq.tile([P, SIZES[g] * P, PACK], BF16, align_bytes=64)
             words = grouped[:].rearrange("q c t -> q (c t)").bitcast(F32).rearrange("q (c u) -> q c u", u=2)
-            for pair in range(GROUP // 2):
+            for pair in range(SIZES[g] // 2):
                 bank = psum.tile([P, 2, 2, P], F32, tag="bank")
                 for u in range(2):
                     for a in range(2):
@@ -146,8 +188,8 @@ def tile_mdn_pa_t_kernel(tc, x, W1, b1, Wpi, bpi, Wsig, bsig, Wmu, bmu, out_0, o
             x_grouped[g] = grouped
 
         def quantise_x(g):
-            codes = xq.tile([P, COLS], U32, align_bytes=64)
-            scales = xq.tile([P, COLS], U8, align_bytes=64)
+            codes = xq.tile([P, SIZES[g] * P], U32, align_bytes=64)
+            scales = xq.tile([P, SIZES[g] * P], U8, align_bytes=64)
             nc.vector.quantize_mx(
                 out=codes[:].bitcast(FP8X4),
                 scales=scales[:],
@@ -158,9 +200,9 @@ def tile_mdn_pa_t_kernel(tc, x, W1, b1, Wpi, bpi, Wsig, bsig, Wmu, bmu, out_0, o
         def hidden_bank(g, t):
             codes, scales = x_mx[g]
             if t == 0:
-                planes = zq.tile([P, PACK, COLS], BF16)
+                planes = zq.tile([P, PACK, SIZES[g] * P], BF16)
                 z_planes[g] = planes
-            bank = psum.tile([P, COLS], F32, tag="bank")
+            bank = psum.tile([P, SIZES[g] * P], F32, tag="bank")
             nc.tensor.matmul_mx(
                 out=bank[:],
                 lhsT=w1_codes[:, t * P : (t + 1) * P].bitcast(FP8X4),
@@ -172,8 +214,12 @@ def tile_mdn_pa_t_kernel(tc, x, W1, b1, Wpi, bpi, Wsig, bsig, Wmu, bmu, out_0, o
             )
             nc.scalar.activation(out=z_planes[g][:, t, :], in_=bank[:], func=ACT.Tanh, bias=b1_col[:, t : t + 1])
 
-        def regroup_z(g):
-            grouped = zq.tile([P, COLS, PACK], BF16, align_bytes=64)
+        def regroup_z(g, engine="g"):
+            grouped = zq.tile([P, SIZES[g] * P, PACK], BF16, align_bytes=64)
+            if engine == "v":
+                nc.vector.tensor_copy(out=grouped[:], in_=z_planes[g][:].rearrange("m t c -> m c t"))
+                z_grouped[g] = grouped
+                return
             nc.gpsimd.tensor_scalar(
                 out=grouped[:],
                 in0=z_planes[g][:].rearrange("m t c -> m c t"),
@@ -185,8 +231,8 @@ def tile_mdn_pa_t_kernel(tc, x, W1, b1, Wpi, bpi, Wsig, bsig, Wmu, bmu, out_0, o
             z_grouped[g] = grouped
 
         def quantise_z(g):
-            codes = zq.tile([P, COLS], U32, align_bytes=64)
-            scales = zq.tile([P, COLS], U8, align_bytes=64)
+            codes = zq.tile([P, SIZES[g] * P], U32, align_bytes=64)
+            scales = zq.tile([P, SIZES[g] * P], U8, align_bytes=64)
             nc.vector.quantize_mx(
                 out=codes[:].bitcast(FP8X4),
                 scales=scales[:],
@@ -197,7 +243,7 @@ def tile_mdn_pa_t_kernel(tc, x, W1, b1, Wpi, bpi, Wsig, bsig, Wmu, bmu, out_0, o
         def logit_bank(g, pair):
             codes, scales = z_mx[g]
             if pair == 0:
-                logit = outs.tile([P, GROUP, COMP], F32)
+                logit = outs.tile([P, SIZES[g], COMP], F32)
                 logits[g] = logit
             bank = psum.tile([P, 2, COMP], F32, tag="bank")
             for a in range(2):
@@ -219,45 +265,84 @@ def tile_mdn_pa_t_kernel(tc, x, W1, b1, Wpi, bpi, Wsig, bsig, Wmu, bmu, out_0, o
             )
 
         def row_max(g):
-            negated = small.tile([P, GROUP], F32)
+            negated = small.tile([P, SIZES[g]], F32)
             nc.vector.tensor_reduce(out=negated[:], in_=logits[g][:], axis=AXIS.X, op=ALU.max, negate=True)
             neg_max[g] = negated
 
-        def sd_and_mu(g):
+        def sd_bank(g, a):
             codes, scales = z_mx[g]
-            rows = slice(g * GROUP, (g + 1) * GROUP)
-            sd = zq.tile([P, KD // P, COLS], F32)
-            mu_sb = outs.tile([P, GROUP, KD], F32)
-            for a in range(GROUP):
-                cols = slice(a * P, (a + 1) * P)
-                bank = psum.tile([P, COLS], F32, tag="bank")
-                nc.tensor.matmul_mx(
-                    out=bank[:],
-                    lhsT=wsig_codes[:, cols].bitcast(FP8X4),
-                    lhsT_scale=wsig_scales[:, cols],
-                    rhs=codes[:].bitcast(FP8X4),
-                    rhs_scale=scales[:],
-                    start=True,
-                    stop=True,
-                )
-                nc.scalar.activation(out=sd[:, a, :], in_=bank[:], func=ACT.Exp, bias=bsig_col[:, a : a + 1])
-                bank = psum.tile([P, KD], F32, tag="bank")
-                nc.tensor.matmul_mx(
-                    out=bank[:],
-                    lhsT=codes[:, cols].bitcast(FP8X4),
-                    lhsT_scale=scales[:, cols],
-                    rhs=wmu_codes[:].bitcast(FP8X4),
-                    rhs_scale=wmu_scales[:],
-                    start=True,
-                    stop=True,
-                )
-                nc.vector.tensor_tensor(out=mu_sb[:, a, :], in0=bank[:], in1=bmu_row[:], op=ALU.add)
-            nc.sync.dma_start(out=mu_view[:, rows, :], in_=mu_sb[:])
-            sd_t[g] = sd
+            size = SIZES[g]
+            half = size // 2 * P
+            if a == 0:
+                sd = zq.tile([P, KD // P, half], F32)
+                sd_t[g] = sd
+            cols = slice(a * P, (a + 1) * P)
+            bank = psum.tile([P, half], F32, tag="bank")
+            nc.tensor.matmul_mx(
+                out=bank[:],
+                lhsT=wsig_codes[:, cols].bitcast(FP8X4),
+                lhsT_scale=wsig_scales[:, cols],
+                rhs=codes[:, :half].bitcast(FP8X4),
+                rhs_scale=scales[:, :half],
+                start=True,
+                stop=True,
+            )
+            nc.scalar.activation(out=sd_t[g][:, a, :], in_=bank[:], func=ACT.Exp, bias=bsig_col[:, a : a + 1])
+
+        def sd_rows(g, a):
+            codes, scales = z_mx[g]
+            cols = slice(a * P, (a + 1) * P)
+            bank = psum.tile([P, KD], F32, tag="bank")
+            nc.tensor.matmul_mx(
+                out=bank[:],
+                lhsT=codes[:, cols].bitcast(FP8X4),
+                lhsT_scale=scales[:, cols],
+                rhs=wsig_codes[:].bitcast(FP8X4),
+                rhs_scale=wsig_scales[:],
+                start=True,
+                stop=True,
+            )
+            row = rows_pool.tile([P, KD], F32)
+            nc.vector.tensor_tensor(out=row[:], in0=bank[:], in1=bsig_row[:], op=ALU.add)
+            nc.scalar.activation(out=row[:], in_=row[:], func=ACT.Exp)
+            sd_row[g, a] = row
+
+        def place_sigma(g, a):
+            diag = diagonals[(FIRSTS[g] + a) % len(diagonals)]
+            nc.gpsimd.tensor_scalar(
+                out=diag[:].rearrange("r (k q) -> r k q", q=4)[:, :, ::3],
+                in0=sd_row[g, a][:].rearrange("r (k i) -> r k i", i=2),
+                scalar1=1.0,
+                scalar2=0.0,
+                op0=ALU.mult,
+                op1=ALU.add,
+            )
+            nc.sync.dma_start(out=sigma_view[:, FIRSTS[g] + a, :], in_=diag[:])
+
+        def mu_bank(g, a):
+            codes, scales = z_mx[g]
+            if a % 2 == 0:
+                mu_sb = outs.tile([P, 2, KD], F32)
+                mu_out[g] = mu_sb
+            cols = slice(a * P, (a + 1) * P)
+            bank = psum.tile([P, KD], F32, tag="bank")
+            nc.tensor.matmul_mx(
+                out=bank[:],
+                lhsT=codes[:, cols].bitcast(FP8X4),
+                lhsT_scale=scales[:, cols],
+                rhs=wmu_codes[:].bitcast(FP8X4),
+                rhs_scale=wmu_scales[:],
+                start=True,
+                stop=True,
+            )
+            nc.vector.tensor_tensor(out=mu_out[g][:, a % 2, :], in0=bank[:], in1=bmu_row[:], op=ALU.add)
+            if a % 2 == 1:
+                rows = slice(FIRSTS[g] + a - 1, FIRSTS[g] + a + 1)
+                nc.sync.dma_start(out=mu_view[:, rows, :], in_=mu_out[g][:])
 
         def exp_pi(g):
-            total = small.tile([P, GROUP], F32)
-            for a in range(GROUP):
+            total = small.tile([P, SIZES[g]], F32)
+            for a in range(SIZES[g]):
                 nc.scalar.activation(
                     out=logits[g][:, a, :],
                     in_=logits[g][:, a, :],
@@ -268,9 +353,9 @@ def tile_mdn_pa_t_kernel(tc, x, W1, b1, Wpi, bpi, Wsig, bsig, Wmu, bmu, out_0, o
             sums[g] = total
 
         def finish_pi(g):
-            inverse = small.tile([P, GROUP], F32)
+            inverse = small.tile([P, SIZES[g]], F32)
             nc.vector.reciprocal(out=inverse[:], in_=sums[g][:])
-            for a in range(GROUP):
+            for a in range(SIZES[g]):
                 nc.gpsimd.tensor_scalar(
                     out=logits[g][:, a, :],
                     in0=logits[g][:, a, :],
@@ -279,30 +364,26 @@ def tile_mdn_pa_t_kernel(tc, x, W1, b1, Wpi, bpi, Wsig, bsig, Wmu, bmu, out_0, o
                     op0=ALU.mult,
                     op1=ALU.add,
                 )
-            nc.sync.dma_start(out=pi_view[:, g * GROUP : (g + 1) * GROUP, :], in_=logits[g][:])
+            nc.sync.dma_start(out=pi_view[:, FIRSTS[g] : FIRSTS[g] + SIZES[g], :], in_=logits[g][:])
 
-        def spread_sigma(g):
-            for pair in range(GROUP // 2):
-                sigma_sb = sig_pool.tile([P, 2, DIAG], F32)
-                for a in range(2):
-                    cols = slice((2 * pair + a) * P, (2 * pair + a + 1) * P)
-                    for half in range(2):
-                        bank = psum.tile([P, 2, 2 * P], F32, tag="bank")
-                        for b in range(2):
-                            for side in range(2):
-                                nc.tensor.transpose(
-                                    out=bank[:, b, side * P : (side + 1) * P],
-                                    in_=sd_t[g][:, 2 * half + b, cols],
-                                    identity=spread[:, side * P : (side + 1) * P],
-                                )
-                        dest = sigma_sb[:, a, half * 4 * P : (half + 1) * 4 * P]
-                        number = 4 * pair + 2 * a + half
-                        if number not in SCALAR_BANKS:
-                            nc.vector.tensor_copy(out=dest, in_=bank[:].rearrange("r b n -> r (b n)"))
-                        else:
-                            nc.scalar.copy(out=dest, in_=bank[:].rearrange("r b n -> r (b n)"))
-                first = g * GROUP + 2 * pair
-                nc.sync.dma_start(out=sigma_view[:, first : first + 2, :], in_=sigma_sb[:])
+        def spread_sigma(g, a):
+            sigma_sb = sig_pool.tile([P, DIAG], F32)
+            cols = slice(a * P, (a + 1) * P)
+            for half in range(2):
+                bank = psum.tile([P, 2, 2 * P], F32, tag="bank")
+                for b in range(2):
+                    for side in range(2):
+                        nc.tensor.transpose(
+                            out=bank[:, b, side * P : (side + 1) * P],
+                            in_=sd_t[g][:, 2 * half + b, cols],
+                            identity=spread[:, side * P : (side + 1) * P],
+                        )
+                dest = sigma_sb[:, half * 4 * P : (half + 1) * 4 * P]
+                if half == 1:
+                    nc.vector.tensor_copy(out=dest, in_=bank[:].rearrange("r b n -> r (b n)"))
+                else:
+                    nc.scalar.copy(out=dest, in_=bank[:].rearrange("r b n -> r (b n)"))
+            nc.sync.dma_start(out=sigma_view[:, FIRSTS[g] + a, :], in_=sigma_sb[:])
 
         def live(g):
             return 0 <= g < GROUPS
@@ -311,30 +392,70 @@ def tile_mdn_pa_t_kernel(tc, x, W1, b1, Wpi, bpi, Wsig, bsig, Wmu, bmu, out_0, o
         transpose_x(0)
         quantise_w1()
         quantise_x(0)
+        hidden_bank(0, 0)
+        hidden_bank(0, 1)
+        hidden_bank(0, 2)
+        hidden_bank(0, 3)
+        regroup_head_weight("mu", wmu_raw, KD, "g")
+        regroup_head_weight("sig", wsig_raw, KD, "g")
+        spread_bias(bmu_row, KD, KD)
         transpose_x(1)
-        for step in range(GROUPS + 1):
-            for t in range(PACK):
-                if live(step):
-                    hidden_bank(step, t)
-                if t < GROUP // 2 and live(step - 1):
+        regroup_z(0, "v")
+        quantise_z(0)
+        quantise_head_weight("mu", wmu_codes, wmu_scales)
+        quantise_x(1)
+        spread_bias(bsig_row, 0, KD)
+        spread_bias(bpi_row, 2 * KD, COMP)
+        turn_bias()
+        regroup_head_weight("pi", wpi_raw, COMP, "v")
+        quantise_head_weight("pi", wpi_codes, wpi_scales)
+        quantise_head_weight("sig", wsig_codes, wsig_scales)
+        transpose_x(2)
+        for step in range(1, GROUPS + 1):
+            tiles = range(SIZES[step - 1])
+            spread_tiles = tiles[: len(tiles) // 2]
+            placed_tiles = tiles[len(tiles) // 2 :]
+
+            if step < GROUPS:
+                hidden_bank(step, 0)
+            if step <= 1:
+                for a in tiles:
+                    mu_bank(step - 1, a)
+                    if step < GROUPS and a < 3:
+                        hidden_bank(step, a + 1)
+                if step < GROUPS:
+                    for t in range(len(tiles) + 1, PACK):
+                        hidden_bank(step, t)
+                for t in range(len(tiles) // 2):
                     logit_bank(step - 1, t)
-            if step == 0:
-                quantise_head_weight(wpi_raw, COMP, wpi_codes, wpi_scales)
-                quantise_head_weight(wsig_raw, KD, wsig_codes, wsig_scales)
-            if live(step - 1):
-                row_max(step - 1)
-                sd_and_mu(step - 1)
-                exp_pi(step - 1)
-            if live(step):
-                regroup_z(step)
-            if live(step + 1):
+            else:
+                for t in range(len(tiles) // 2):
+                    logit_bank(step - 1, t)
+                    if step < GROUPS:
+                        hidden_bank(step, t + 1)
+                if step < GROUPS:
+                    for t in range(len(tiles) // 2 + 1, PACK):
+                        hidden_bank(step, t)
+            for a in placed_tiles:
+                sd_rows(step - 1, a)
+            row_max(step - 1)
+            for a in range(KD // P):
+                sd_bank(step - 1, a)
+                if a in tiles and step > 1:
+                    mu_bank(step - 1, a)
+            exp_pi(step - 1)
+            if step < GROUPS:
+                regroup_z(step, "g" if step == 1 else "g")
+            for a in placed_tiles:
+                place_sigma(step - 1, a)
+            if step + 1 < GROUPS:
                 quantise_x(step + 1)
-            if live(step):
+            if step < GROUPS and 1:
                 quantise_z(step)
-            if step == 0:
-                quantise_head_weight(wmu_raw, KD, wmu_codes, wmu_scales)
-            if live(step - 1):
-                finish_pi(step - 1)
-                spread_sigma(step - 1)
-            if live(step + 2):
+            for a in spread_tiles:
+                spread_sigma(step - 1, a)
+            if step < GROUPS and not 1:
+                quantise_z(step)
+            finish_pi(step - 1)
+            if step + 2 < GROUPS:
                 transpose_x(step + 2)

@@ -88,11 +88,11 @@ def tile_mdn_pa_t_kernel(tc, x, W1, b1, Wpi, bpi, Wsig, bsig, Wmu, bmu, out_0, o
                 in_=ident[:].rearrange("c (k i) -> c k i", i=2)[:, :, i],
             )
 
-        diagonals = []
+        sd_planes = []
         for i in range(4):
-            diag = const.tile([P, DIAG], F32, name=f"diag{i}")
-            nc.gpsimd.memset(diag[:], 0.0)
-            diagonals.append(diag)
+            plane = const.tile([P, 4, COMP], F32, name=f"planes{i}")
+            nc.gpsimd.memset(plane[:, 1:3, :], 0.0)
+            sd_planes.append(plane)
 
         ones = const.tile([P, P], BF16)
         nc.vector.memset(ones[:], 1.0)
@@ -304,20 +304,25 @@ def tile_mdn_pa_t_kernel(tc, x, W1, b1, Wpi, bpi, Wsig, bsig, Wmu, bmu, out_0, o
             )
             row = rows_pool.tile([P, KD], F32)
             nc.vector.tensor_tensor(out=row[:], in0=bank[:], in1=bsig_row[:], op=ALU.add)
-            nc.scalar.activation(out=row[:], in_=row[:], func=ACT.Exp)
-            sd_row[g, a] = row
+            planes = sd_planes[(FIRSTS[g] + a) % len(sd_planes)]
+            nc.scalar.activation(
+                out=planes[:, ::3, :],
+                in_=row[:].rearrange("r (k i) -> r i k", i=2),
+                func=ACT.Exp,
+            )
+            sd_row[g, a] = planes
 
         def place_sigma(g, a):
-            diag = diagonals[(FIRSTS[g] + a) % len(diagonals)]
+            sigma_sb = sig_pool.tile([P, DIAG], F32)
             nc.gpsimd.tensor_scalar(
-                out=diag[:].rearrange("r (k q) -> r k q", q=4)[:, :, ::3],
-                in0=sd_row[g, a][:].rearrange("r (k i) -> r k i", i=2),
+                out=sigma_sb[:].rearrange("r (k q) -> r k q", q=4),
+                in0=sd_row[g, a][:].rearrange("r q k -> r k q"),
                 scalar1=1.0,
                 scalar2=0.0,
                 op0=ALU.mult,
                 op1=ALU.add,
             )
-            nc.sync.dma_start(out=sigma_view[:, FIRSTS[g] + a, :], in_=diag[:])
+            nc.sync.dma_start(out=sigma_view[:, FIRSTS[g] + a, :], in_=sigma_sb[:])
 
         def mu_bank(g, a):
             codes, scales = z_mx[g]

@@ -272,7 +272,7 @@ def tile_mdn_pa_t_kernel(tc, x, W1, b1, Wpi, bpi, Wsig, bsig, Wmu, bmu, out_0, o
         def sd_bank(g, a):
             codes, scales = z_mx[g]
             size = SIZES[g]
-            half = size // 2 * P
+            half = size * P
             if a == 0:
                 sd = zq.tile([P, KD // P, half], F32)
                 sd_t[g] = sd
@@ -384,7 +384,7 @@ def tile_mdn_pa_t_kernel(tc, x, W1, b1, Wpi, bpi, Wsig, bsig, Wmu, bmu, out_0, o
                             identity=spread[:, side * P : (side + 1) * P],
                         )
                 dest = sigma_sb[:, half * 4 * P : (half + 1) * 4 * P]
-                if half == 1:
+                if half == 1 or a == 3:
                     nc.vector.tensor_copy(out=dest, in_=bank[:].rearrange("r b n -> r (b n)"))
                 else:
                     nc.scalar.copy(out=dest, in_=bank[:].rearrange("r b n -> r (b n)"))
@@ -418,8 +418,8 @@ def tile_mdn_pa_t_kernel(tc, x, W1, b1, Wpi, bpi, Wsig, bsig, Wmu, bmu, out_0, o
         transpose_x(2)
         for step in range(1, GROUPS + 1):
             tiles = range(SIZES[step - 1])
-            spread_tiles = tiles[: len(tiles) // 2]
-            placed_tiles = tiles[len(tiles) // 2 :]
+            spread_tiles = tiles
+            placed_tiles = tiles[:0]
 
             if step < GROUPS:
                 hidden_bank(step, 0)

@@ -45,7 +45,6 @@ def tile_mdn_pa_t_kernel(tc, x, W1, b1, Wpi, bpi, Wsig, bsig, Wmu, bmu, out_0, o
         small = ctx.enter_context(tc.tile_pool(name="small", bufs=3))
         outs = ctx.enter_context(tc.tile_pool(name="outs", bufs=3))
         sig_pool = ctx.enter_context(tc.tile_pool(name="sig", bufs=8))
-        rows_pool = ctx.enter_context(tc.tile_pool(name="rows", bufs=4))
         psum = ctx.enter_context(tc.psum_pool(name="psum", bufs=8))
 
         x_sb = {}
@@ -88,15 +87,8 @@ def tile_mdn_pa_t_kernel(tc, x, W1, b1, Wpi, bpi, Wsig, bsig, Wmu, bmu, out_0, o
                 in_=ident[:].rearrange("c (k i) -> c k i", i=2)[:, :, i],
             )
 
-        sd_planes = []
-        for i in range(4):
-            plane = const.tile([P, 4, COMP], F32, name=f"planes{i}")
-            nc.gpsimd.memset(plane[:, 1:3, :], 0.0)
-            sd_planes.append(plane)
-
         ones = const.tile([P, P], BF16)
         nc.vector.memset(ones[:], 1.0)
-        bsig_row = const.tile([P, KD], BF16)
         bmu_row = const.tile([P, KD], BF16)
         bpi_row = const.tile([P, COMP], BF16)
         bsig_col = const.tile([P, KD // P], F32)
@@ -167,7 +159,6 @@ def tile_mdn_pa_t_kernel(tc, x, W1, b1, Wpi, bpi, Wsig, bsig, Wmu, bmu, out_0, o
         sums = {}
         sd_t = {}
         mu_out = {}
-        sd_row = {}
 
         def transpose_x(g):
             grouped = xq.tile([P, SIZES[g] * P, PACK], BF16, align_bytes=64)
@@ -289,41 +280,6 @@ def tile_mdn_pa_t_kernel(tc, x, W1, b1, Wpi, bpi, Wsig, bsig, Wmu, bmu, out_0, o
             )
             nc.scalar.activation(out=sd_t[g][:, a, :], in_=bank[:], func=ACT.Exp, bias=bsig_col[:, a : a + 1])
 
-        def sd_rows(g, a):
-            codes, scales = z_mx[g]
-            cols = slice(a * P, (a + 1) * P)
-            bank = psum.tile([P, KD], F32, tag="bank")
-            nc.tensor.matmul_mx(
-                out=bank[:],
-                lhsT=codes[:, cols].bitcast(FP8X4),
-                lhsT_scale=scales[:, cols],
-                rhs=wsig_codes[:].bitcast(FP8X4),
-                rhs_scale=wsig_scales[:],
-                start=True,
-                stop=True,
-            )
-            row = rows_pool.tile([P, KD], F32)
-            nc.vector.tensor_tensor(out=row[:], in0=bank[:], in1=bsig_row[:], op=ALU.add)
-            planes = sd_planes[(FIRSTS[g] + a) % len(sd_planes)]
-            nc.scalar.activation(
-                out=planes[:, ::3, :],
-                in_=row[:].rearrange("r (k i) -> r i k", i=2),
-                func=ACT.Exp,
-            )
-            sd_row[g, a] = planes
-
-        def place_sigma(g, a):
-            sigma_sb = sig_pool.tile([P, DIAG], F32)
-            nc.gpsimd.tensor_scalar(
-                out=sigma_sb[:].rearrange("r (k q) -> r k q", q=4),
-                in0=sd_row[g, a][:].rearrange("r q k -> r k q"),
-                scalar1=1.0,
-                scalar2=0.0,
-                op0=ALU.mult,
-                op1=ALU.add,
-            )
-            nc.sync.dma_start(out=sigma_view[:, FIRSTS[g] + a, :], in_=sigma_sb[:])
-
         def mu_bank(g, a):
             codes, scales = z_mx[g]
             if a % 2 == 0:
@@ -384,7 +340,7 @@ def tile_mdn_pa_t_kernel(tc, x, W1, b1, Wpi, bpi, Wsig, bsig, Wmu, bmu, out_0, o
                             identity=spread[:, side * P : (side + 1) * P],
                         )
                 dest = sigma_sb[:, half * 4 * P : (half + 1) * 4 * P]
-                if half == 1 or a == 3:
+                if half == 1 or a == 0:
                     nc.vector.tensor_copy(out=dest, in_=bank[:].rearrange("r b n -> r (b n)"))
                 else:
                     nc.scalar.copy(out=dest, in_=bank[:].rearrange("r b n -> r (b n)"))
@@ -401,15 +357,14 @@ def tile_mdn_pa_t_kernel(tc, x, W1, b1, Wpi, bpi, Wsig, bsig, Wmu, bmu, out_0, o
         hidden_bank(0, 1)
         hidden_bank(0, 2)
         hidden_bank(0, 3)
-        regroup_head_weight("mu", wmu_raw, KD, "g")
-        regroup_head_weight("sig", wsig_raw, KD, "g")
-        spread_bias(bmu_row, KD, KD)
         transpose_x(1)
+        regroup_head_weight("mu", wmu_raw, KD, "v")
+        spread_bias(bmu_row, KD, KD)
         regroup_z(0, "v")
         quantise_z(0)
         quantise_head_weight("mu", wmu_codes, wmu_scales)
         quantise_x(1)
-        spread_bias(bsig_row, 0, KD)
+        regroup_head_weight("sig", wsig_raw, KD, "v")
         spread_bias(bpi_row, 2 * KD, COMP)
         turn_bias()
         regroup_head_weight("pi", wpi_raw, COMP, "v")
@@ -418,8 +373,6 @@ def tile_mdn_pa_t_kernel(tc, x, W1, b1, Wpi, bpi, Wsig, bsig, Wmu, bmu, out_0, o
         transpose_x(2)
         for step in range(1, GROUPS + 1):
             tiles = range(SIZES[step - 1])
-            spread_tiles = tiles
-            placed_tiles = tiles[:0]
 
             if step < GROUPS:
                 hidden_bank(step, 0)
@@ -441,8 +394,6 @@ def tile_mdn_pa_t_kernel(tc, x, W1, b1, Wpi, bpi, Wsig, bsig, Wmu, bmu, out_0, o
                 if step < GROUPS:
                     for t in range(len(tiles) // 2 + 1, PACK):
                         hidden_bank(step, t)
-            for a in placed_tiles:
-                sd_rows(step - 1, a)
             row_max(step - 1)
             for a in range(KD // P):
                 sd_bank(step - 1, a)
@@ -451,16 +402,14 @@ def tile_mdn_pa_t_kernel(tc, x, W1, b1, Wpi, bpi, Wsig, bsig, Wmu, bmu, out_0, o
             exp_pi(step - 1)
             if step < GROUPS:
                 regroup_z(step, "g" if step == 1 else "g")
-            for a in placed_tiles:
-                place_sigma(step - 1, a)
+            for a in tiles[:1]:
+                spread_sigma(step - 1, a)
             if step + 1 < GROUPS:
                 quantise_x(step + 1)
-            if step < GROUPS and 1:
+            if step < GROUPS:
                 quantise_z(step)
-            for a in spread_tiles:
+            for a in tiles[1:]:
                 spread_sigma(step - 1, a)
-            if step < GROUPS and not 1:
-                quantise_z(step)
             finish_pi(step - 1)
             if step + 2 < GROUPS:
                 transpose_x(step + 2)

@@ -14,6 +14,7 @@ AXIS = mybir.AxisListType
 
 P = 128
 PACK = 4
+RUN = 4
 BATCH = 4096
 COND = 512
 HID = 512
@@ -121,24 +122,28 @@ def tile_mdn_pa_t_kernel(tc, x, W1, b1, Wpi, bpi, Wsig, bsig, Wmu, bmu, out_0, o
 
         w_staged = {}
 
-        def quantise_w1():
-            w1_grouped = wstage.tile([P, PACK, P, PACK], BF16, align_bytes=64, tag="w_grouped")
-            nc.vector.tensor_copy(out=w1_grouped[:], in_=w1_raw[:].rearrange("q j (m t) -> q t m j", t=PACK))
-            nc.vector.quantize_mx(
-                out=w1_codes[:].bitcast(FP8X4),
-                scales=w1_scales[:],
-                in_=w1_grouped[:].rearrange("q t m j -> q (t m j)"),
+        w1_grouped = const.tile([P, PACK, P, PACK], BF16, align_bytes=64)
+
+        def regroup_w1(t):
+            nc.vector.tensor_copy(
+                out=w1_grouped[:, t, :, :].rearrange("q (c i) j -> q c j i", i=RUN),
+                in_=w1_raw[:].rearrange("q j (c i t) -> q t c j i", i=RUN, t=PACK)[:, t, :, :, :],
             )
 
-        def regroup_head_weight(name, raw, width, engine):
+        def quantise_w1(t):
+            cols = slice(t * P, (t + 1) * P)
+            nc.vector.quantize_mx(
+                out=w1_codes[:, cols].bitcast(FP8X4),
+                scales=w1_scales[:, cols],
+                in_=w1_grouped[:, t, :, :].rearrange("q m j -> q (m j)"),
+            )
+
+        def regroup_head_weight(name, raw, width):
             w_grouped = wstage.tile([P, width, PACK], BF16, align_bytes=64, tag="w_grouped")
-            view = raw[:].rearrange("p j n -> p n j")
-            if engine == "v":
-                nc.vector.tensor_copy(out=w_grouped[:], in_=view)
-            elif engine == "s":
-                nc.scalar.copy(out=w_grouped[:], in_=view)
-            else:
-                nc.gpsimd.tensor_scalar(out=w_grouped[:], in0=view, scalar1=1.0, scalar2=0.0, op0=ALU.mult, op1=ALU.add)
+            nc.vector.tensor_copy(
+                out=w_grouped[:].rearrange("p (c i) j -> p c j i", i=RUN),
+                in_=raw[:].rearrange("p j (c i) -> p c j i", i=RUN),
+            )
             w_staged[name] = w_grouped
 
         def quantise_head_weight(name, codes, scales):
@@ -208,12 +213,15 @@ def tile_mdn_pa_t_kernel(tc, x, W1, b1, Wpi, bpi, Wsig, bsig, Wmu, bmu, out_0, o
         def regroup_z(g, engine="g"):
             grouped = zq.tile([P, SIZES[g] * P, PACK], BF16, align_bytes=64)
             if engine == "v":
-                nc.vector.tensor_copy(out=grouped[:], in_=z_planes[g][:].rearrange("m t c -> m c t"))
+                nc.vector.tensor_copy(
+                    out=grouped[:].rearrange("m (c i) t -> m c t i", i=RUN),
+                    in_=z_planes[g][:].rearrange("m t (c i) -> m c t i", i=RUN),
+                )
                 z_grouped[g] = grouped
                 return
             nc.gpsimd.tensor_scalar(
-                out=grouped[:],
-                in0=z_planes[g][:].rearrange("m t c -> m c t"),
+                out=grouped[:].rearrange("m (c i) t -> m c t i", i=RUN),
+                in0=z_planes[g][:].rearrange("m t (c i) -> m c t i", i=RUN),
                 scalar1=1.0,
                 scalar2=0.0,
                 op0=ALU.mult,
@@ -351,23 +359,26 @@ def tile_mdn_pa_t_kernel(tc, x, W1, b1, Wpi, bpi, Wsig, bsig, Wmu, bmu, out_0, o
 
         ctx.enter_context(tc.manual_schedule())
         transpose_x(0)
-        quantise_w1()
-        quantise_x(0)
-        hidden_bank(0, 0)
-        hidden_bank(0, 1)
-        hidden_bank(0, 2)
-        hidden_bank(0, 3)
+        regroup_w1(0)
+        for t in range(1, PACK):
+            regroup_w1(t)
+            quantise_w1(t - 1)
+            if t == 1:
+                quantise_x(0)
+            hidden_bank(0, t - 1)
+        quantise_w1(PACK - 1)
+        hidden_bank(0, PACK - 1)
         transpose_x(1)
-        regroup_head_weight("mu", wmu_raw, KD, "v")
+        regroup_head_weight("mu", wmu_raw, KD)
         spread_bias(bmu_row, KD, KD)
         regroup_z(0, "v")
         quantise_z(0)
         quantise_head_weight("mu", wmu_codes, wmu_scales)
         quantise_x(1)
-        regroup_head_weight("sig", wsig_raw, KD, "v")
+        regroup_head_weight("sig", wsig_raw, KD)
         spread_bias(bpi_row, 2 * KD, COMP)
         turn_bias()
-        regroup_head_weight("pi", wpi_raw, COMP, "v")
+        regroup_head_weight("pi", wpi_raw, COMP)
         quantise_head_weight("pi", wpi_codes, wpi_scales)
         quantise_head_weight("sig", wsig_codes, wsig_scales)
         transpose_x(2)
@@ -401,7 +412,7 @@ def tile_mdn_pa_t_kernel(tc, x, W1, b1, Wpi, bpi, Wsig, bsig, Wmu, bmu, out_0, o
                     mu_bank(step - 1, a)
             exp_pi(step - 1)
             if step < GROUPS:
-                regroup_z(step, "g" if step == 1 else "g")
+                regroup_z(step, "g")
             for a in tiles[:1]:
                 spread_sigma(step - 1, a)
             if step + 1 < GROUPS:

@@ -26,6 +26,7 @@ TILES = BATCH // P
 SIZES = (2, 4, 4, 4, 4, 4, 4, 4, 2)
 FIRSTS = tuple(sum(SIZES[:g]) for g in range(len(SIZES)))
 GROUPS = len(SIZES)
+PLACED = 1
 
 FLOPS = 2 * BATCH * (COND * HID + HID * (COMP + 2 * KD))
 
@@ -46,6 +47,7 @@ def tile_mdn_pa_t_kernel(tc, x, W1, b1, Wpi, bpi, Wsig, bsig, Wmu, bmu, out_0, o
         small = ctx.enter_context(tc.tile_pool(name="small", bufs=3))
         outs = ctx.enter_context(tc.tile_pool(name="outs", bufs=3))
         sig_pool = ctx.enter_context(tc.tile_pool(name="sig", bufs=8))
+        rows_pool = ctx.enter_context(tc.tile_pool(name="rows", bufs=4))
         psum = ctx.enter_context(tc.psum_pool(name="psum", bufs=8))
 
         x_sb = {}
@@ -88,8 +90,15 @@ def tile_mdn_pa_t_kernel(tc, x, W1, b1, Wpi, bpi, Wsig, bsig, Wmu, bmu, out_0, o
                 in_=ident[:].rearrange("c (k i) -> c k i", i=2)[:, :, i],
             )
 
+        sd_planes = []
+        for i in range(2):
+            plane = const.tile([P, 4, COMP], F32, name=f"planes{i}")
+            nc.gpsimd.memset(plane[:, 1:3, :], 0.0)
+            sd_planes.append(plane)
+
         ones = const.tile([P, P], BF16)
         nc.vector.memset(ones[:], 1.0)
+        bsig_row = const.tile([P, KD], BF16)
         bmu_row = const.tile([P, KD], BF16)
         bpi_row = const.tile([P, COMP], BF16)
         bsig_col = const.tile([P, KD // P], F32)
@@ -164,6 +173,7 @@ def tile_mdn_pa_t_kernel(tc, x, W1, b1, Wpi, bpi, Wsig, bsig, Wmu, bmu, out_0, o
         sums = {}
         sd_t = {}
         mu_out = {}
+        sd_row = {}
 
         def transpose_x(g):
             grouped = xq.tile([P, SIZES[g] * P, PACK], BF16, align_bytes=64)
@@ -220,8 +230,8 @@ def tile_mdn_pa_t_kernel(tc, x, W1, b1, Wpi, bpi, Wsig, bsig, Wmu, bmu, out_0, o
                 z_grouped[g] = grouped
                 return
             nc.gpsimd.tensor_scalar(
-                out=grouped[:].rearrange("m (c i) t -> m c t i", i=RUN),
-                in0=z_planes[g][:].rearrange("m t (c i) -> m c t i", i=RUN),
+                out=grouped[:],
+                in0=z_planes[g][:].rearrange("m t c -> m c t"),
                 scalar1=1.0,
                 scalar2=0.0,
                 op0=ALU.mult,
@@ -286,7 +296,41 @@ def tile_mdn_pa_t_kernel(tc, x, W1, b1, Wpi, bpi, Wsig, bsig, Wmu, bmu, out_0, o
                 start=True,
                 stop=True,
             )
-            nc.scalar.activation(out=sd_t[g][:, a, :], in_=bank[:], func=ACT.Exp, bias=bsig_col[:, a : a + 1])
+            skip = PLACED * P if size == 4 else 0
+            nc.scalar.activation(
+                out=sd_t[g][:, a, skip:], in_=bank[:, skip:], func=ACT.Exp, bias=bsig_col[:, a : a + 1]
+            )
+
+        def sd_rows(g, a):
+            codes, scales = z_mx[g]
+            cols = slice(a * P, (a + 1) * P)
+            bank = psum.tile([P, KD], F32, tag="bank")
+            nc.tensor.matmul_mx(
+                out=bank[:],
+                lhsT=codes[:, cols].bitcast(FP8X4),
+                lhsT_scale=scales[:, cols],
+                rhs=wsig_codes[:].bitcast(FP8X4),
+                rhs_scale=wsig_scales[:],
+                start=True,
+                stop=True,
+            )
+            row = rows_pool.tile([P, KD], F32)
+            nc.vector.tensor_tensor(out=row[:], in0=bank[:], in1=bsig_row[:], op=ALU.add)
+            planes = sd_planes[g % len(sd_planes)]
+            nc.scalar.activation(
+                out=planes[:, ::3, :],
+                in_=row[:].rearrange("r (k i) -> r i k", i=2),
+                func=ACT.Exp,
+            )
+            sd_row[g, a] = planes
+
+        def place_sigma(g, a):
+            sigma_sb = sig_pool.tile([P, DIAG], F32)
+            nc.vector.tensor_copy(
+                out=sigma_sb[:].rearrange("r (k q) -> r k q", q=4),
+                in_=sd_row[g, a][:].rearrange("r q k -> r k q"),
+            )
+            nc.sync.dma_start(out=sigma_view[:, FIRSTS[g] + a, :], in_=sigma_sb[:])
 
         def mu_bank(g, a):
             codes, scales = z_mx[g]
@@ -348,14 +392,11 @@ def tile_mdn_pa_t_kernel(tc, x, W1, b1, Wpi, bpi, Wsig, bsig, Wmu, bmu, out_0, o
                             identity=spread[:, side * P : (side + 1) * P],
                         )
                 dest = sigma_sb[:, half * 4 * P : (half + 1) * 4 * P]
-                if half == 1 or a == 0:
+                if half == 1:
                     nc.vector.tensor_copy(out=dest, in_=bank[:].rearrange("r b n -> r (b n)"))
                 else:
                     nc.scalar.copy(out=dest, in_=bank[:].rearrange("r b n -> r (b n)"))
             nc.sync.dma_start(out=sigma_view[:, FIRSTS[g] + a, :], in_=sigma_sb[:])
-
-        def live(g):
-            return 0 <= g < GROUPS
 
         ctx.enter_context(tc.manual_schedule())
         transpose_x(0)
@@ -371,6 +412,7 @@ def tile_mdn_pa_t_kernel(tc, x, W1, b1, Wpi, bpi, Wsig, bsig, Wmu, bmu, out_0, o
         transpose_x(1)
         regroup_head_weight("mu", wmu_raw, KD)
         spread_bias(bmu_row, KD, KD)
+        spread_bias(bsig_row, 0, KD)
         regroup_z(0, "v")
         quantise_z(0)
         quantise_head_weight("mu", wmu_codes, wmu_scales)
@@ -382,45 +424,60 @@ def tile_mdn_pa_t_kernel(tc, x, W1, b1, Wpi, bpi, Wsig, bsig, Wmu, bmu, out_0, o
         quantise_head_weight("pi", wpi_codes, wpi_scales)
         quantise_head_weight("sig", wsig_codes, wsig_scales)
         transpose_x(2)
+        quantise_x(2)
+        transpose_x(3)
         for step in range(1, GROUPS + 1):
-            tiles = range(SIZES[step - 1])
-
-            if step < GROUPS:
+            g = step - 1
+            size = SIZES[g]
+            nxt = step < GROUPS
+            rows = PLACED if size == 4 else 0
+            if nxt:
                 hidden_bank(step, 0)
-            if step <= 1:
-                for a in tiles:
-                    mu_bank(step - 1, a)
-                    if step < GROUPS and a < 3:
-                        hidden_bank(step, a + 1)
-                if step < GROUPS:
-                    for t in range(len(tiles) + 1, PACK):
-                        hidden_bank(step, t)
-                for t in range(len(tiles) // 2):
-                    logit_bank(step - 1, t)
-            else:
-                for t in range(len(tiles) // 2):
-                    logit_bank(step - 1, t)
-                    if step < GROUPS:
-                        hidden_bank(step, t + 1)
-                if step < GROUPS:
-                    for t in range(len(tiles) // 2 + 1, PACK):
-                        hidden_bank(step, t)
-            row_max(step - 1)
-            for a in range(KD // P):
-                sd_bank(step - 1, a)
-                if a in tiles and step > 1:
-                    mu_bank(step - 1, a)
-            exp_pi(step - 1)
-            if step < GROUPS:
-                regroup_z(step, "g")
-            for a in tiles[:1]:
-                spread_sigma(step - 1, a)
-            if step + 1 < GROUPS:
-                quantise_x(step + 1)
-            if step < GROUPS:
+            if g == 0:
+                for a in range(size):
+                    mu_bank(g, a)
+            if 0 < size // 2:
+                logit_bank(g, 0)
+            if nxt:
+                hidden_bank(step, 1)
+            if 1 < size // 2:
+                logit_bank(g, 1)
+            if nxt:
+                hidden_bank(step, 2)
+            if nxt:
+                hidden_bank(step, 3)
+            for a in range(rows):
+                sd_rows(g, a)
+            row_max(g)
+            sd_bank(g, 0)
+            if 0 < g and 0 < size:
+                mu_bank(g, 0)
+            sd_bank(g, 1)
+            if 0 < g and 1 < size:
+                mu_bank(g, 1)
+            sd_bank(g, 2)
+            if 0 < g and 2 < size:
+                mu_bank(g, 2)
+            sd_bank(g, 3)
+            if 0 < g and 3 < size:
+                mu_bank(g, 3)
+            exp_pi(g)
+            if nxt:
+                regroup_z(step)
+            if rows <= 0 < size:
+                spread_sigma(g, 0)
+            if rows <= 1 < size:
+                spread_sigma(g, 1)
+            if nxt:
                 quantise_z(step)
-            for a in tiles[1:]:
-                spread_sigma(step - 1, a)
-            finish_pi(step - 1)
             if step + 2 < GROUPS:
-                transpose_x(step + 2)
+                quantise_x(step + 2)
+            for a in range(rows):
+                place_sigma(g, a)
+            if rows <= 2 < size:
+                spread_sigma(g, 2)
+            finish_pi(g)
+            if rows <= 3 < size:
+                spread_sigma(g, 3)
+            if step + 3 < GROUPS:
+                transpose_x(step + 3)

@@ -23,10 +23,11 @@ KD = 512
 DIAG = 4 * COMP
 
 TILES = BATCH // P
+FULL = 4
 SIZES = (2, 4, 4, 4, 4, 4, 4, 4, 2)
 FIRSTS = tuple(sum(SIZES[:g]) for g in range(len(SIZES)))
 GROUPS = len(SIZES)
-PLACED = 1
+FINE = 1
 
 FLOPS = 2 * BATCH * (COND * HID + HID * (COMP + 2 * KD))
 
@@ -40,29 +41,30 @@ def tile_mdn_pa_t_kernel(tc, x, W1, b1, Wpi, bpi, Wsig, bsig, Wmu, bmu, out_0, o
 
     with ExitStack() as ctx:
         const = ctx.enter_context(tc.tile_pool(name="const", bufs=1))
-        wstage = ctx.enter_context(tc.tile_pool(name="wstage", bufs=4))
-        xpool = ctx.enter_context(tc.tile_pool(name="xpool", bufs=GROUPS))
         xq = ctx.enter_context(tc.tile_pool(name="xq", bufs=4))
         zq = ctx.enter_context(tc.tile_pool(name="zq", bufs=2))
         small = ctx.enter_context(tc.tile_pool(name="small", bufs=3))
+        rows = ctx.enter_context(tc.tile_pool(name="rows", bufs=2))
         outs = ctx.enter_context(tc.tile_pool(name="outs", bufs=3))
-        sig_pool = ctx.enter_context(tc.tile_pool(name="sig", bufs=8))
-        rows_pool = ctx.enter_context(tc.tile_pool(name="rows", bufs=4))
+        sig_pool = ctx.enter_context(tc.tile_pool(name="sig", bufs=5))
         psum = ctx.enter_context(tc.psum_pool(name="psum", bufs=8))
 
         x_sb = {}
 
-        def load_x(g):
-            x_g = xpool.tile([P, SIZES[g], COND], BF16)
-            nc.sync.dma_start(out=x_g[:], in_=x_view[:, FIRSTS[g] : FIRSTS[g] + SIZES[g], :])
-            x_sb[g] = x_g
+        def load_x(g, count):
+            tiles = sum(SIZES[g : g + count])
+            x_g = const.tile([P, tiles, COND], BF16, name=f"x_{g}")
+            nc.sync.dma_start(out=x_g[:], in_=x_view[:, FIRSTS[g] : FIRSTS[g] + tiles, :])
+            for h in range(g, g + count):
+                first = FIRSTS[h] - FIRSTS[g]
+                x_sb[h] = x_g[:, first : first + SIZES[h], :]
 
         w1_raw = const.tile([P, PACK, HID], BF16)
         nc.sync.dma_start(
             out=w1_raw[:].rearrange("q (u e) n -> q u e n", u=2),
             in_=W1.rearrange("(u q e) n -> q u e n", u=2, e=2),
         )
-        load_x(0)
+        load_x(0, 1)
         b1_col = const.tile([P, PACK], BF16)
         nc.sync.dma_start(out=b1_col[:], in_=b1.rearrange("(m t) -> m t", t=PACK))
         bias_rows = const.tile([P, 2 * KD + COMP], BF16)
@@ -72,13 +74,13 @@ def tile_mdn_pa_t_kernel(tc, x, W1, b1, Wpi, bpi, Wsig, bsig, Wmu, bmu, out_0, o
         nc.sync.dma_start(out=bias_rows[0:1, 2 * KD :], in_=bpi.rearrange("(o n) -> o n", o=1))
         wmu_raw = const.tile([P, PACK, KD], BF16)
         nc.sync.dma_start(out=wmu_raw[:], in_=Wmu.rearrange("(p j) n -> p j n", j=PACK))
-        load_x(1)
+        load_x(1, 1)
         wsig_raw = const.tile([P, PACK, KD], BF16)
         nc.sync.dma_start(out=wsig_raw[:], in_=Wsig.rearrange("(p j) n -> p j n", j=PACK))
         wpi_raw = const.tile([P, PACK, COMP], BF16)
         nc.sync.dma_start(out=wpi_raw[:], in_=Wpi.rearrange("(p j) n -> p j n", j=PACK))
-        for g in range(2, GROUPS):
-            load_x(g)
+        for g in range(2, GROUPS, 1):
+            load_x(g, min(1, GROUPS - g))
 
         ident = const.tile([P, P], F32)
         make_identity(nc, ident[:])
@@ -89,10 +91,9 @@ def tile_mdn_pa_t_kernel(tc, x, W1, b1, Wpi, bpi, Wsig, bsig, Wmu, bmu, out_0, o
                 out=spread[:].rearrange("c (k q) -> c k q", q=4)[:, :, 3 * i],
                 in_=ident[:].rearrange("c (k i) -> c k i", i=2)[:, :, i],
             )
-
         sd_planes = []
         for i in range(2):
-            plane = const.tile([P, 4, COMP], F32, name=f"planes{i}")
+            plane = const.tile([P, 4, COMP], F32, name=f"planes_{i}")
             nc.gpsimd.memset(plane[:, 1:3, :], 0.0)
             sd_planes.append(plane)
 
@@ -120,18 +121,9 @@ def tile_mdn_pa_t_kernel(tc, x, W1, b1, Wpi, bpi, Wsig, bsig, Wmu, bmu, out_0, o
                 )
             nc.scalar.copy(out=bsig_col[:], in_=bank[:])
 
+        w1_grouped = const.tile([P, PACK, P, PACK], BF16, align_bytes=64)
         w1_codes = const.tile([P, HID], U32, align_bytes=64)
         w1_scales = const.tile([P, HID], U8, align_bytes=64)
-        wpi_codes = const.tile([P, COMP], U32, align_bytes=64)
-        wpi_scales = const.tile([P, COMP], U8, align_bytes=64)
-        wmu_codes = const.tile([P, KD], U32, align_bytes=64)
-        wmu_scales = const.tile([P, KD], U8, align_bytes=64)
-        wsig_codes = const.tile([P, KD], U32, align_bytes=64)
-        wsig_scales = const.tile([P, KD], U8, align_bytes=64)
-
-        w_staged = {}
-
-        w1_grouped = const.tile([P, PACK, P, PACK], BF16, align_bytes=64)
 
         def regroup_w1(t):
             nc.vector.tensor_copy(
@@ -147,21 +139,30 @@ def tile_mdn_pa_t_kernel(tc, x, W1, b1, Wpi, bpi, Wsig, bsig, Wmu, bmu, out_0, o
                 in_=w1_grouped[:, t, :, :].rearrange("q m j -> q (m j)"),
             )
 
-        def regroup_head_weight(name, raw, width):
-            w_grouped = wstage.tile([P, width, PACK], BF16, align_bytes=64, tag="w_grouped")
+        def head_weight(name, raw, width):
+            grouped = const.tile([P, width, PACK], BF16, align_bytes=64, name=f"{name}_grouped")
+            codes = const.tile([P, width], U32, align_bytes=64, name=f"{name}_codes")
+            scales = const.tile([P, width], U8, align_bytes=64, name=f"{name}_scales")
+            return raw, grouped, codes, scales
+
+        def regroup_weight(weight):
+            raw, grouped, codes, scales = weight
             nc.vector.tensor_copy(
-                out=w_grouped[:].rearrange("p (c i) j -> p c j i", i=RUN),
+                out=grouped[:].rearrange("p (c i) j -> p c j i", i=RUN),
                 in_=raw[:].rearrange("p j (c i) -> p c j i", i=RUN),
             )
-            w_staged[name] = w_grouped
 
-        def quantise_head_weight(name, codes, scales):
-            w_grouped = w_staged[name]
+        def quantise_weight(weight):
+            raw, grouped, codes, scales = weight
             nc.vector.quantize_mx(
                 out=codes[:].bitcast(FP8X4),
                 scales=scales[:],
-                in_=w_grouped[:].rearrange("p n j -> p (n j)"),
+                in_=grouped[:].rearrange("p n j -> p (n j)"),
             )
+
+        wpi = head_weight("wpi", wpi_raw, COMP)
+        wsig = head_weight("wsig", wsig_raw, KD)
+        wmu = head_weight("wmu", wmu_raw, KD)
 
         x_grouped = {}
         x_mx = {}
@@ -173,7 +174,22 @@ def tile_mdn_pa_t_kernel(tc, x, W1, b1, Wpi, bpi, Wsig, bsig, Wmu, bmu, out_0, o
         sums = {}
         sd_t = {}
         mu_out = {}
-        sd_row = {}
+        sigma_out = {}
+
+        def product(bank, stationary, moving):
+            nc.tensor.matmul_mx(
+                out=bank,
+                lhsT=stationary[0].bitcast(FP8X4),
+                lhsT_scale=stationary[1],
+                rhs=moving[0].bitcast(FP8X4),
+                rhs_scale=moving[1],
+                start=True,
+                stop=True,
+            )
+
+        def columns(operand, a, count=1):
+            cols = slice(a * P, (a + count) * P)
+            return operand[0][:, cols], operand[1][:, cols]
 
         def transpose_x(g):
             grouped = xq.tile([P, SIZES[g] * P, PACK], BF16, align_bytes=64)
@@ -204,39 +220,29 @@ def tile_mdn_pa_t_kernel(tc, x, W1, b1, Wpi, bpi, Wsig, bsig, Wmu, bmu, out_0, o
             x_mx[g] = (codes, scales)
 
         def hidden_bank(g, t):
-            codes, scales = x_mx[g]
             if t == 0:
                 planes = zq.tile([P, PACK, SIZES[g] * P], BF16)
                 z_planes[g] = planes
             bank = psum.tile([P, SIZES[g] * P], F32, tag="bank")
-            nc.tensor.matmul_mx(
-                out=bank[:],
-                lhsT=w1_codes[:, t * P : (t + 1) * P].bitcast(FP8X4),
-                lhsT_scale=w1_scales[:, t * P : (t + 1) * P],
-                rhs=codes[:].bitcast(FP8X4),
-                rhs_scale=scales[:],
-                start=True,
-                stop=True,
-            )
+            product(bank[:], columns((w1_codes, w1_scales), t), columns(x_mx[g], 0, SIZES[g]))
             nc.scalar.activation(out=z_planes[g][:, t, :], in_=bank[:], func=ACT.Tanh, bias=b1_col[:, t : t + 1])
 
-        def regroup_z(g, engine="g"):
+        def regroup_z(g):
             grouped = zq.tile([P, SIZES[g] * P, PACK], BF16, align_bytes=64)
-            if engine == "v":
+            if g == 0:
                 nc.vector.tensor_copy(
                     out=grouped[:].rearrange("m (c i) t -> m c t i", i=RUN),
                     in_=z_planes[g][:].rearrange("m t (c i) -> m c t i", i=RUN),
                 )
-                z_grouped[g] = grouped
-                return
-            nc.gpsimd.tensor_scalar(
-                out=grouped[:],
-                in0=z_planes[g][:].rearrange("m t c -> m c t"),
-                scalar1=1.0,
-                scalar2=0.0,
-                op0=ALU.mult,
-                op1=ALU.add,
-            )
+            else:
+                nc.gpsimd.tensor_scalar(
+                    out=grouped[:],
+                    in0=z_planes[g][:].rearrange("m t c -> m c t"),
+                    scalar1=1.0,
+                    scalar2=0.0,
+                    op0=ALU.mult,
+                    op1=ALU.add,
+                )
             z_grouped[g] = grouped
 
         def quantise_z(g):
@@ -250,22 +256,12 @@ def tile_mdn_pa_t_kernel(tc, x, W1, b1, Wpi, bpi, Wsig, bsig, Wmu, bmu, out_0, o
             z_mx[g] = (codes, scales)
 
         def logit_bank(g, pair):
-            codes, scales = z_mx[g]
             if pair == 0:
                 logit = outs.tile([P, SIZES[g], COMP], F32)
                 logits[g] = logit
             bank = psum.tile([P, 2, COMP], F32, tag="bank")
             for a in range(2):
-                cols = slice((2 * pair + a) * P, (2 * pair + a + 1) * P)
-                nc.tensor.matmul_mx(
-                    out=bank[:, a, :],
-                    lhsT=codes[:, cols].bitcast(FP8X4),
-                    lhsT_scale=scales[:, cols],
-                    rhs=wpi_codes[:].bitcast(FP8X4),
-                    rhs_scale=wpi_scales[:],
-                    start=True,
-                    stop=True,
-                )
+                product(bank[:, a, :], columns(z_mx[g], 2 * pair + a), columns(wpi[2:], 0, COMP // P))
             nc.vector.tensor_tensor(
                 out=logits[g][:, 2 * pair : 2 * pair + 2, :],
                 in0=bank[:],
@@ -277,81 +273,6 @@ def tile_mdn_pa_t_kernel(tc, x, W1, b1, Wpi, bpi, Wsig, bsig, Wmu, bmu, out_0, o
             negated = small.tile([P, SIZES[g]], F32)
             nc.vector.tensor_reduce(out=negated[:], in_=logits[g][:], axis=AXIS.X, op=ALU.max, negate=True)
             neg_max[g] = negated
-
-        def sd_bank(g, a):
-            codes, scales = z_mx[g]
-            size = SIZES[g]
-            half = size * P
-            if a == 0:
-                sd = zq.tile([P, KD // P, half], F32)
-                sd_t[g] = sd
-            cols = slice(a * P, (a + 1) * P)
-            bank = psum.tile([P, half], F32, tag="bank")
-            nc.tensor.matmul_mx(
-                out=bank[:],
-                lhsT=wsig_codes[:, cols].bitcast(FP8X4),
-                lhsT_scale=wsig_scales[:, cols],
-                rhs=codes[:, :half].bitcast(FP8X4),
-                rhs_scale=scales[:, :half],
-                start=True,
-                stop=True,
-            )
-            skip = PLACED * P if size == 4 else 0
-            nc.scalar.activation(
-                out=sd_t[g][:, a, skip:], in_=bank[:, skip:], func=ACT.Exp, bias=bsig_col[:, a : a + 1]
-            )
-
-        def sd_rows(g, a):
-            codes, scales = z_mx[g]
-            cols = slice(a * P, (a + 1) * P)
-            bank = psum.tile([P, KD], F32, tag="bank")
-            nc.tensor.matmul_mx(
-                out=bank[:],
-                lhsT=codes[:, cols].bitcast(FP8X4),
-                lhsT_scale=scales[:, cols],
-                rhs=wsig_codes[:].bitcast(FP8X4),
-                rhs_scale=wsig_scales[:],
-                start=True,
-                stop=True,
-            )
-            row = rows_pool.tile([P, KD], F32)
-            nc.vector.tensor_tensor(out=row[:], in0=bank[:], in1=bsig_row[:], op=ALU.add)
-            planes = sd_planes[g % len(sd_planes)]
-            nc.scalar.activation(
-                out=planes[:, ::3, :],
-                in_=row[:].rearrange("r (k i) -> r i k", i=2),
-                func=ACT.Exp,
-            )
-            sd_row[g, a] = planes
-
-        def place_sigma(g, a):
-            sigma_sb = sig_pool.tile([P, DIAG], F32)
-            nc.vector.tensor_copy(
-                out=sigma_sb[:].rearrange("r (k q) -> r k q", q=4),
-                in_=sd_row[g, a][:].rearrange("r q k -> r k q"),
-            )
-            nc.sync.dma_start(out=sigma_view[:, FIRSTS[g] + a, :], in_=sigma_sb[:])
-
-        def mu_bank(g, a):
-            codes, scales = z_mx[g]
-            if a % 2 == 0:
-                mu_sb = outs.tile([P, 2, KD], F32)
-                mu_out[g] = mu_sb
-            cols = slice(a * P, (a + 1) * P)
-            bank = psum.tile([P, KD], F32, tag="bank")
-            nc.tensor.matmul_mx(
-                out=bank[:],
-                lhsT=codes[:, cols].bitcast(FP8X4),
-                lhsT_scale=scales[:, cols],
-                rhs=wmu_codes[:].bitcast(FP8X4),
-                rhs_scale=wmu_scales[:],
-                start=True,
-                stop=True,
-            )
-            nc.vector.tensor_tensor(out=mu_out[g][:, a % 2, :], in0=bank[:], in1=bmu_row[:], op=ALU.add)
-            if a % 2 == 1:
-                rows = slice(FIRSTS[g] + a - 1, FIRSTS[g] + a + 1)
-                nc.sync.dma_start(out=mu_view[:, rows, :], in_=mu_out[g][:])
 
         def exp_pi(g):
             total = small.tile([P, SIZES[g]], F32)
@@ -377,10 +298,53 @@ def tile_mdn_pa_t_kernel(tc, x, W1, b1, Wpi, bpi, Wsig, bsig, Wmu, bmu, out_0, o
                     op0=ALU.mult,
                     op1=ALU.add,
                 )
+
+        def store_pi(g):
             nc.sync.dma_start(out=pi_view[:, FIRSTS[g] : FIRSTS[g] + SIZES[g], :], in_=logits[g][:])
 
+        def fine(g):
+            return g <= FINE or g == GROUPS - 1
+
+        def mu_bank(g, a):
+            if a == 0:
+                mu_sb = outs.tile([P, SIZES[g], KD], F32)
+                mu_out[g] = mu_sb
+            bank = psum.tile([P, KD], F32, tag="bank")
+            product(bank[:], columns(z_mx[g], a), columns(wmu[2:], 0, KD // P))
+            nc.vector.tensor_tensor(out=mu_out[g][:, a, :], in0=bank[:], in1=bmu_row[:], op=ALU.add)
+            count = 2 if fine(g) else SIZES[g]
+            if (a + 1) % count == 0:
+                first = a + 1 - count
+                nc.sync.dma_start(
+                    out=mu_view[:, FIRSTS[g] + first : FIRSTS[g] + a + 1, :], in_=mu_out[g][:, first : a + 1, :]
+                )
+
+
+        def spread_tiles(g):
+            return SIZES[g] - 1 if SIZES[g] == FULL else SIZES[g]
+
+        def sigma_tile(g, a):
+            if (g, a // 2) not in sigma_out:
+                sigma_pair = sig_pool.tile([P, 2, DIAG], F32)
+                sigma_out[g, a // 2] = sigma_pair
+            return sigma_out[g, a // 2][:, a % 2, :]
+
+        def store_sigma(g, a, count):
+            first = FIRSTS[g] + a
+            nc.sync.dma_start(
+                out=sigma_view[:, first : first + count, :], in_=sigma_out[g, a // 2][:, a % 2 : a % 2 + count, :]
+            )
+
+        def sd_bank(g, a):
+            used = spread_tiles(g) * P
+            if a == 0:
+                sd = zq.tile([P, KD // P, used], F32)
+                sd_t[g] = sd
+            bank = psum.tile([P, SIZES[g] * P], F32, tag="bank")
+            product(bank[:], columns(wsig[2:], a), columns(z_mx[g], 0, SIZES[g]))
+            nc.scalar.activation(out=sd_t[g][:, a, :], in_=bank[:, :used], func=ACT.Exp, bias=bsig_col[:, a : a + 1])
+
         def spread_sigma(g, a):
-            sigma_sb = sig_pool.tile([P, DIAG], F32)
             cols = slice(a * P, (a + 1) * P)
             for half in range(2):
                 bank = psum.tile([P, 2, 2 * P], F32, tag="bank")
@@ -391,12 +355,30 @@ def tile_mdn_pa_t_kernel(tc, x, W1, b1, Wpi, bpi, Wsig, bsig, Wmu, bmu, out_0, o
                             in_=sd_t[g][:, 2 * half + b, cols],
                             identity=spread[:, side * P : (side + 1) * P],
                         )
-                dest = sigma_sb[:, half * 4 * P : (half + 1) * 4 * P]
+                dest = sigma_tile(g, a)[:, half * 4 * P : (half + 1) * 4 * P]
                 if half == 1:
                     nc.vector.tensor_copy(out=dest, in_=bank[:].rearrange("r b n -> r (b n)"))
                 else:
                     nc.scalar.copy(out=dest, in_=bank[:].rearrange("r b n -> r (b n)"))
-            nc.sync.dma_start(out=sigma_view[:, FIRSTS[g] + a, :], in_=sigma_sb[:])
+
+        def sd_rows(g):
+            bank = psum.tile([P, KD], F32, tag="bank")
+            product(bank[:], columns(z_mx[g], SIZES[g] - 1), columns(wsig[2:], 0, KD // P))
+            row = rows.tile([P, KD], F32)
+            nc.vector.tensor_tensor(out=row[:], in0=bank[:], in1=bsig_row[:], op=ALU.add)
+            nc.scalar.activation(
+                out=sd_planes[g % 2][:, ::3, :], in_=row[:].rearrange("r (k i) -> r i k", i=2), func=ACT.Exp
+            )
+
+        def place_sigma(g):
+            nc.gpsimd.tensor_scalar(
+                out=sigma_tile(g, SIZES[g] - 1).rearrange("r (k q) -> r k q", q=4),
+                in0=sd_planes[g % 2][:].rearrange("r q k -> r k q"),
+                scalar1=1.0,
+                scalar2=0.0,
+                op0=ALU.mult,
+                op1=ALU.add,
+            )
 
         ctx.enter_context(tc.manual_schedule())
         transpose_x(0)
@@ -410,74 +392,84 @@ def tile_mdn_pa_t_kernel(tc, x, W1, b1, Wpi, bpi, Wsig, bsig, Wmu, bmu, out_0, o
         quantise_w1(PACK - 1)
         hidden_bank(0, PACK - 1)
         transpose_x(1)
-        regroup_head_weight("mu", wmu_raw, KD)
+        regroup_weight(wmu)
         spread_bias(bmu_row, KD, KD)
-        spread_bias(bsig_row, 0, KD)
-        regroup_z(0, "v")
+        regroup_z(0)
         quantise_z(0)
-        quantise_head_weight("mu", wmu_codes, wmu_scales)
+        quantise_weight(wmu)
         quantise_x(1)
-        regroup_head_weight("sig", wsig_raw, KD)
+        regroup_weight(wsig)
         spread_bias(bpi_row, 2 * KD, COMP)
         turn_bias()
-        regroup_head_weight("pi", wpi_raw, COMP)
-        quantise_head_weight("pi", wpi_codes, wpi_scales)
-        quantise_head_weight("sig", wsig_codes, wsig_scales)
+        spread_bias(bsig_row, 0, KD)
+        regroup_weight(wpi)
+        quantise_weight(wpi)
+        quantise_weight(wsig)
         transpose_x(2)
         quantise_x(2)
         transpose_x(3)
         for step in range(1, GROUPS + 1):
             g = step - 1
             size = SIZES[g]
-            nxt = step < GROUPS
-            rows = PLACED if size == 4 else 0
-            if nxt:
+            full = size == FULL
+            more = step < GROUPS
+            if more:
                 hidden_bank(step, 0)
             if g == 0:
                 for a in range(size):
                     mu_bank(g, a)
-            if 0 < size // 2:
-                logit_bank(g, 0)
-            if nxt:
+            logit_bank(g, 0)
+            if more:
                 hidden_bank(step, 1)
-            if 1 < size // 2:
+            if full:
                 logit_bank(g, 1)
-            if nxt:
+            if more:
                 hidden_bank(step, 2)
-            if nxt:
+            if more:
                 hidden_bank(step, 3)
-            for a in range(rows):
-                sd_rows(g, a)
+            if full:
+                sd_rows(g)
             row_max(g)
             sd_bank(g, 0)
-            if 0 < g and 0 < size:
+            if g > 0 and 0 < size:
                 mu_bank(g, 0)
             sd_bank(g, 1)
-            if 0 < g and 1 < size:
+            if g > 0 and 1 < size:
                 mu_bank(g, 1)
             sd_bank(g, 2)
-            if 0 < g and 2 < size:
+            if g > 0 and 2 < size:
                 mu_bank(g, 2)
             sd_bank(g, 3)
-            if 0 < g and 3 < size:
+            if g > 0 and 3 < size:
                 mu_bank(g, 3)
             exp_pi(g)
-            if nxt:
+            if more:
                 regroup_z(step)
-            if rows <= 0 < size:
+            if 0 < spread_tiles(g):
                 spread_sigma(g, 0)
-            if rows <= 1 < size:
+            if fine(g):
+                store_sigma(g, 0, 1)
+            if 1 < spread_tiles(g):
                 spread_sigma(g, 1)
-            if nxt:
+            if fine(g):
+                store_sigma(g, 1, 1)
+            else:
+                store_sigma(g, 0, 2)
+            if more:
                 quantise_z(step)
             if step + 2 < GROUPS:
                 quantise_x(step + 2)
-            for a in range(rows):
-                place_sigma(g, a)
-            if rows <= 2 < size:
-                spread_sigma(g, 2)
             finish_pi(g)
-            if rows <= 3 < size:
-                spread_sigma(g, 3)
+            if full:
+                place_sigma(g)
+            if 2 < spread_tiles(g):
+                spread_sigma(g, 2)
+                if fine(g):
+                    store_sigma(g, 2, 1)
+            store_pi(g)
+            if full and fine(g):
+                store_sigma(g, 3, 1)
+            elif full:
+                store_sigma(g, 2, 2)
             if step + 3 < GROUPS:
                 transpose_x(step + 3)

from contextlib import ExitStack

import concourse.mybir as mybir
from concourse.masks import make_identity

F32 = mybir.dt.float32
BF16 = mybir.dt.bfloat16
U32 = mybir.dt.uint32
U8 = mybir.dt.uint8
FP8X4 = mybir.dt.float8_e4m3fn_x4
ACT = mybir.ActivationFunctionType
ALU = mybir.AluOpType
AXIS = mybir.AxisListType

P = 128
PACK = 4
RUN = 4
BATCH = 4096
COND = 512
HID = 512
COMP = 256
KD = 512
DIAG = 4 * COMP

TILES = BATCH // P
FULL = 4
SIZES = (2, 4, 4, 4, 4, 4, 4, 4, 2)
FIRSTS = tuple(sum(SIZES[:g]) for g in range(len(SIZES)))
GROUPS = len(SIZES)
FINE = 1

FLOPS = 2 * BATCH * (COND * HID + HID * (COMP + 2 * KD))


def tile_mdn_pa_t_kernel(tc, x, W1, b1, Wpi, bpi, Wsig, bsig, Wmu, bmu, out_0, out_1, out_2):
    nc = tc.nc
    x_view = x.rearrange("(p t) k -> p t k", t=TILES)
    pi_view = out_0.rearrange("(p t) k -> p t k", t=TILES)
    sigma_view = out_1.rearrange("(p t) k i j -> p t (k i j)", t=TILES)
    mu_view = out_2.rearrange("(p t) k d -> p t (k d)", t=TILES)

    with ExitStack() as ctx:
        const = ctx.enter_context(tc.tile_pool(name="const", bufs=1))
        xq = ctx.enter_context(tc.tile_pool(name="xq", bufs=4))
        zq = ctx.enter_context(tc.tile_pool(name="zq", bufs=2))
        small = ctx.enter_context(tc.tile_pool(name="small", bufs=3))
        rows = ctx.enter_context(tc.tile_pool(name="rows", bufs=2))
        outs = ctx.enter_context(tc.tile_pool(name="outs", bufs=3))
        sig_pool = ctx.enter_context(tc.tile_pool(name="sig", bufs=5))
        psum = ctx.enter_context(tc.psum_pool(name="psum", bufs=8))

        x_sb = {}

        def load_x(g, count):
            tiles = sum(SIZES[g : g + count])
            x_g = const.tile([P, tiles, COND], BF16, name=f"x_{g}")
            nc.sync.dma_start(out=x_g[:], in_=x_view[:, FIRSTS[g] : FIRSTS[g] + tiles, :])
            for h in range(g, g + count):
                first = FIRSTS[h] - FIRSTS[g]
                x_sb[h] = x_g[:, first : first + SIZES[h], :]

        w1_raw = const.tile([P, PACK, HID], BF16)
        nc.sync.dma_start(
            out=w1_raw[:].rearrange("q (u e) n -> q u e n", u=2),
            in_=W1.rearrange("(u q e) n -> q u e n", u=2, e=2),
        )
        load_x(0, 1)
        b1_col = const.tile([P, PACK], BF16)
        nc.sync.dma_start(out=b1_col[:], in_=b1.rearrange("(m t) -> m t", t=PACK))
        bias_rows = const.tile([P, 2 * KD + COMP], BF16)
        nc.vector.memset(bias_rows[:], 0.0)
        nc.sync.dma_start(out=bias_rows[0:1, 0:KD], in_=bsig.rearrange("(o n) -> o n", o=1))
        nc.sync.dma_start(out=bias_rows[0:1, KD : 2 * KD], in_=bmu.rearrange("(o n) -> o n", o=1))
        nc.sync.dma_start(out=bias_rows[0:1, 2 * KD :], in_=bpi.rearrange("(o n) -> o n", o=1))
        wmu_raw = const.tile([P, PACK, KD], BF16)
        nc.sync.dma_start(out=wmu_raw[:], in_=Wmu.rearrange("(p j) n -> p j n", j=PACK))
        load_x(1, 1)
        wsig_raw = const.tile([P, PACK, KD], BF16)
        nc.sync.dma_start(out=wsig_raw[:], in_=Wsig.rearrange("(p j) n -> p j n", j=PACK))
        wpi_raw = const.tile([P, PACK, COMP], BF16)
        nc.sync.dma_start(out=wpi_raw[:], in_=Wpi.rearrange("(p j) n -> p j n", j=PACK))
        for g in range(2, GROUPS, 1):
            load_x(g, min(1, GROUPS - g))

        ident = const.tile([P, P], F32)
        make_identity(nc, ident[:])
        spread = const.tile([P, 2 * P], F32)
        nc.vector.memset(spread[:], 0.0)
        for i in range(2):
            nc.vector.tensor_copy(
                out=spread[:].rearrange("c (k q) -> c k q", q=4)[:, :, 3 * i],
                in_=ident[:].rearrange("c (k i) -> c k i", i=2)[:, :, i],
            )
        sd_planes = []
        for i in range(2):
            plane = const.tile([P, 4, COMP], F32, name=f"planes_{i}")
            nc.gpsimd.memset(plane[:, 1:3, :], 0.0)
            sd_planes.append(plane)

        ones = const.tile([P, P], BF16)
        nc.vector.memset(ones[:], 1.0)
        bsig_row = const.tile([P, KD], BF16)
        bmu_row = const.tile([P, KD], BF16)
        bpi_row = const.tile([P, COMP], BF16)
        bsig_col = const.tile([P, KD // P], F32)

        def spread_bias(row, first, width):
            bank = psum.tile([P, width], F32, tag="bank")
            nc.tensor.matmul(out=bank[:], lhsT=ones[:], rhs=bias_rows[:, first : first + width], start=True, stop=True)
            nc.scalar.copy(out=row[:], in_=bank[:])

        def turn_bias():
            bank = psum.tile([P, KD // P], F32, tag="bank")
            for j in range(KD // P):
                nc.tensor.matmul(
                    out=bank[:, j : j + 1],
                    lhsT=bias_rows[:, j * P : (j + 1) * P],
                    rhs=ones[:, 0:1],
                    start=True,
                    stop=True,
                )
            nc.scalar.copy(out=bsig_col[:], in_=bank[:])

        w1_grouped = const.tile([P, PACK, P, PACK], BF16, align_bytes=64)
        w1_codes = const.tile([P, HID], U32, align_bytes=64)
        w1_scales = const.tile([P, HID], U8, align_bytes=64)

        def regroup_w1(t):
            nc.vector.tensor_copy(
                out=w1_grouped[:, t, :, :].rearrange("q (c i) j -> q c j i", i=RUN),
                in_=w1_raw[:].rearrange("q j (c i t) -> q t c j i", i=RUN, t=PACK)[:, t, :, :, :],
            )

        def quantise_w1(t):
            cols = slice(t * P, (t + 1) * P)
            nc.vector.quantize_mx(
                out=w1_codes[:, cols].bitcast(FP8X4),
                scales=w1_scales[:, cols],
                in_=w1_grouped[:, t, :, :].rearrange("q m j -> q (m j)"),
            )

        def head_weight(name, raw, width):
            grouped = const.tile([P, width, PACK], BF16, align_bytes=64, name=f"{name}_grouped")
            codes = const.tile([P, width], U32, align_bytes=64, name=f"{name}_codes")
            scales = const.tile([P, width], U8, align_bytes=64, name=f"{name}_scales")
            return raw, grouped, codes, scales

        def regroup_weight(weight):
            raw, grouped, codes, scales = weight
            nc.vector.tensor_copy(
                out=grouped[:].rearrange("p (c i) j -> p c j i", i=RUN),
                in_=raw[:].rearrange("p j (c i) -> p c j i", i=RUN),
            )

        def quantise_weight(weight):
            raw, grouped, codes, scales = weight
            nc.vector.quantize_mx(
                out=codes[:].bitcast(FP8X4),
                scales=scales[:],
                in_=grouped[:].rearrange("p n j -> p (n j)"),
            )

        wpi = head_weight("wpi", wpi_raw, COMP)
        wsig = head_weight("wsig", wsig_raw, KD)
        wmu = head_weight("wmu", wmu_raw, KD)

        x_grouped = {}
        x_mx = {}
        z_planes = {}
        z_grouped = {}
        z_mx = {}
        logits = {}
        neg_max = {}
        sums = {}
        sd_t = {}
        mu_out = {}
        sigma_out = {}

        def product(bank, stationary, moving):
            nc.tensor.matmul_mx(
                out=bank,
                lhsT=stationary[0].bitcast(FP8X4),
                lhsT_scale=stationary[1],
                rhs=moving[0].bitcast(FP8X4),
                rhs_scale=moving[1],
                start=True,
                stop=True,
            )

        def columns(operand, a, count=1):
            cols = slice(a * P, (a + count) * P)
            return operand[0][:, cols], operand[1][:, cols]

        def transpose_x(g):
            grouped = xq.tile([P, SIZES[g] * P, PACK], BF16, align_bytes=64)
            words = grouped[:].rearrange("q c t -> q (c t)").bitcast(F32).rearrange("q (c u) -> q c u", u=2)
            for pair in range(SIZES[g] // 2):
                bank = psum.tile([P, 2, 2, P], F32, tag="bank")
                for u in range(2):
                    for a in range(2):
                        nc.tensor.transpose(
                            out=bank[:, u, a, :],
                            in_=x_sb[g][:, 2 * pair + a, :].bitcast(F32)[:, u * P : (u + 1) * P],
                            identity=ident[:],
                        )
                nc.scalar.copy(
                    out=words[:, pair * 2 * P : (pair + 1) * 2 * P, :],
                    in_=bank[:].rearrange("q u a r -> q (a r) u"),
                )
            x_grouped[g] = grouped

        def quantise_x(g):
            codes = xq.tile([P, SIZES[g] * P], U32, align_bytes=64)
            scales = xq.tile([P, SIZES[g] * P], U8, align_bytes=64)
            nc.vector.quantize_mx(
                out=codes[:].bitcast(FP8X4),
                scales=scales[:],
                in_=x_grouped[g][:].rearrange("q c t -> q (c t)"),
            )
            x_mx[g] = (codes, scales)

        def hidden_bank(g, t):
            if t == 0:
                planes = zq.tile([P, PACK, SIZES[g] * P], BF16)
                z_planes[g] = planes
            bank = psum.tile([P, SIZES[g] * P], F32, tag="bank")
            product(bank[:], columns((w1_codes, w1_scales), t), columns(x_mx[g], 0, SIZES[g]))
            nc.scalar.activation(out=z_planes[g][:, t, :], in_=bank[:], func=ACT.Tanh, bias=b1_col[:, t : t + 1])

        def regroup_z(g):
            grouped = zq.tile([P, SIZES[g] * P, PACK], BF16, align_bytes=64)
            if g == 0:
                nc.vector.tensor_copy(
                    out=grouped[:].rearrange("m (c i) t -> m c t i", i=RUN),
                    in_=z_planes[g][:].rearrange("m t (c i) -> m c t i", i=RUN),
                )
            else:
                nc.gpsimd.tensor_scalar(
                    out=grouped[:],
                    in0=z_planes[g][:].rearrange("m t c -> m c t"),
                    scalar1=1.0,
                    scalar2=0.0,
                    op0=ALU.mult,
                    op1=ALU.add,
                )
            z_grouped[g] = grouped

        def quantise_z(g):
            codes = zq.tile([P, SIZES[g] * P], U32, align_bytes=64)
            scales = zq.tile([P, SIZES[g] * P], U8, align_bytes=64)
            nc.vector.quantize_mx(
                out=codes[:].bitcast(FP8X4),
                scales=scales[:],
                in_=z_grouped[g][:].rearrange("m c t -> m (c t)"),
            )
            z_mx[g] = (codes, scales)

        def logit_bank(g, pair):
            if pair == 0:
                logit = outs.tile([P, SIZES[g], COMP], F32)
                logits[g] = logit
            bank = psum.tile([P, 2, COMP], F32, tag="bank")
            for a in range(2):
                product(bank[:, a, :], columns(z_mx[g], 2 * pair + a), columns(wpi[2:], 0, COMP // P))
            nc.vector.tensor_tensor(
                out=logits[g][:, 2 * pair : 2 * pair + 2, :],
                in0=bank[:],
                in1=bpi_row[:].unsqueeze(1).to_broadcast([P, 2, COMP]),
                op=ALU.add,
            )

        def row_max(g):
            negated = small.tile([P, SIZES[g]], F32)
            nc.vector.tensor_reduce(out=negated[:], in_=logits[g][:], axis=AXIS.X, op=ALU.max, negate=True)
            neg_max[g] = negated

        def exp_pi(g):
            total = small.tile([P, SIZES[g]], F32)
            for a in range(SIZES[g]):
                nc.scalar.activation(
                    out=logits[g][:, a, :],
                    in_=logits[g][:, a, :],
                    func=ACT.Exp,
                    bias=neg_max[g][:, a : a + 1],
                    accum_out=total[:, a : a + 1],
                )
            sums[g] = total

        def finish_pi(g):
            inverse = small.tile([P, SIZES[g]], F32)
            nc.vector.reciprocal(out=inverse[:], in_=sums[g][:])
            for a in range(SIZES[g]):
                nc.gpsimd.tensor_scalar(
                    out=logits[g][:, a, :],
                    in0=logits[g][:, a, :],
                    scalar1=inverse[:, a : a + 1],
                    scalar2=0.0,
                    op0=ALU.mult,
                    op1=ALU.add,
                )

        def store_pi(g):
            nc.sync.dma_start(out=pi_view[:, FIRSTS[g] : FIRSTS[g] + SIZES[g], :], in_=logits[g][:])

        def fine(g):
            return g <= FINE or g == GROUPS - 1

        def mu_bank(g, a):
            if a == 0:
                mu_sb = outs.tile([P, SIZES[g], KD], F32)
                mu_out[g] = mu_sb
            bank = psum.tile([P, KD], F32, tag="bank")
            product(bank[:], columns(z_mx[g], a), columns(wmu[2:], 0, KD // P))
            nc.vector.tensor_tensor(out=mu_out[g][:, a, :], in0=bank[:], in1=bmu_row[:], op=ALU.add)
            count = 2 if fine(g) else SIZES[g]
            if (a + 1) % count == 0:
                first = a + 1 - count
                nc.sync.dma_start(
                    out=mu_view[:, FIRSTS[g] + first : FIRSTS[g] + a + 1, :], in_=mu_out[g][:, first : a + 1, :]
                )


        def spread_tiles(g):
            return SIZES[g] - 1 if SIZES[g] == FULL else SIZES[g]

        def sigma_tile(g, a):
            if (g, a // 2) not in sigma_out:
                sigma_pair = sig_pool.tile([P, 2, DIAG], F32)
                sigma_out[g, a // 2] = sigma_pair
            return sigma_out[g, a // 2][:, a % 2, :]

        def store_sigma(g, a, count):
            first = FIRSTS[g] + a
            nc.sync.dma_start(
                out=sigma_view[:, first : first + count, :], in_=sigma_out[g, a // 2][:, a % 2 : a % 2 + count, :]
            )

        def sd_bank(g, a):
            used = spread_tiles(g) * P
            if a == 0:
                sd = zq.tile([P, KD // P, used], F32)
                sd_t[g] = sd
            bank = psum.tile([P, SIZES[g] * P], F32, tag="bank")
            product(bank[:], columns(wsig[2:], a), columns(z_mx[g], 0, SIZES[g]))
            nc.scalar.activation(out=sd_t[g][:, a, :], in_=bank[:, :used], func=ACT.Exp, bias=bsig_col[:, a : a + 1])

        def spread_sigma(g, a):
            cols = slice(a * P, (a + 1) * P)
            for half in range(2):
                bank = psum.tile([P, 2, 2 * P], F32, tag="bank")
                for b in range(2):
                    for side in range(2):
                        nc.tensor.transpose(
                            out=bank[:, b, side * P : (side + 1) * P],
                            in_=sd_t[g][:, 2 * half + b, cols],
                            identity=spread[:, side * P : (side + 1) * P],
                        )
                dest = sigma_tile(g, a)[:, half * 4 * P : (half + 1) * 4 * P]
                if half == 1:
                    nc.vector.tensor_copy(out=dest, in_=bank[:].rearrange("r b n -> r (b n)"))
                else:
                    nc.scalar.copy(out=dest, in_=bank[:].rearrange("r b n -> r (b n)"))

        def sd_rows(g):
            bank = psum.tile([P, KD], F32, tag="bank")
            product(bank[:], columns(z_mx[g], SIZES[g] - 1), columns(wsig[2:], 0, KD // P))
            row = rows.tile([P, KD], F32)
            nc.vector.tensor_tensor(out=row[:], in0=bank[:], in1=bsig_row[:], op=ALU.add)
            nc.scalar.activation(
                out=sd_planes[g % 2][:, ::3, :], in_=row[:].rearrange("r (k i) -> r i k", i=2), func=ACT.Exp
            )

        def place_sigma(g):
            nc.gpsimd.tensor_scalar(
                out=sigma_tile(g, SIZES[g] - 1).rearrange("r (k q) -> r k q", q=4),
                in0=sd_planes[g % 2][:].rearrange("r q k -> r k q"),
                scalar1=1.0,
                scalar2=0.0,
                op0=ALU.mult,
                op1=ALU.add,
            )

        ctx.enter_context(tc.manual_schedule())
        transpose_x(0)
        regroup_w1(0)
        for t in range(1, PACK):
            regroup_w1(t)
            quantise_w1(t - 1)
            if t == 1:
                quantise_x(0)
            hidden_bank(0, t - 1)
        quantise_w1(PACK - 1)
        hidden_bank(0, PACK - 1)
        transpose_x(1)
        regroup_weight(wmu)
        spread_bias(bmu_row, KD, KD)
        regroup_z(0)
        quantise_z(0)
        quantise_weight(wmu)
        quantise_x(1)
        regroup_weight(wsig)
        spread_bias(bpi_row, 2 * KD, COMP)
        turn_bias()
        spread_bias(bsig_row, 0, KD)
        regroup_weight(wpi)
        quantise_weight(wpi)
        quantise_weight(wsig)
        transpose_x(2)
        quantise_x(2)
        transpose_x(3)
        for step in range(1, GROUPS + 1):
            g = step - 1
            size = SIZES[g]
            full = size == FULL
            more = step < GROUPS
            if more:
                hidden_bank(step, 0)
            if g == 0:
                for a in range(size):
                    mu_bank(g, a)
            logit_bank(g, 0)
            if more:
                hidden_bank(step, 1)
            if full:
                logit_bank(g, 1)
            if more:
                hidden_bank(step, 2)
            if more:
                hidden_bank(step, 3)
            if full:
                sd_rows(g)
            row_max(g)
            sd_bank(g, 0)
            if g > 0 and 0 < size:
                mu_bank(g, 0)
            sd_bank(g, 1)
            if g > 0 and 1 < size:
                mu_bank(g, 1)
            sd_bank(g, 2)
            if g > 0 and 2 < size:
                mu_bank(g, 2)
            sd_bank(g, 3)
            if g > 0 and 3 < size:
                mu_bank(g, 3)
            exp_pi(g)
            if more:
                regroup_z(step)
            if 0 < spread_tiles(g):
                spread_sigma(g, 0)
            if fine(g):
                store_sigma(g, 0, 1)
            if 1 < spread_tiles(g):
                spread_sigma(g, 1)
            if fine(g):
                store_sigma(g, 1, 1)
            else:
                store_sigma(g, 0, 2)
            if more:
                quantise_z(step)
            if step + 2 < GROUPS:
                quantise_x(step + 2)
            finish_pi(g)
            if full:
                place_sigma(g)
            if 2 < spread_tiles(g):
                spread_sigma(g, 2)
                if fine(g):
                    store_sigma(g, 2, 1)
            store_pi(g)
            if full and fine(g):
                store_sigma(g, 3, 1)
            elif full:
                store_sigma(g, 2, 2)
            if step + 3 < GROUPS:
                transpose_x(step + 3)
